import numpy as np
import ml_dtypes


def mxq(x, axis, fmt="e4m3"):
    dtype, down = {"e4m3": (ml_dtypes.float8_e4m3fn, 7), "e5m2": (ml_dtypes.float8_e5m2, 14)}[fmt]
    v = np.moveaxis(np.asarray(x, np.float32).astype(ml_dtypes.bfloat16).astype(np.float64), axis, -1)
    blocks = v.reshape(v.shape[:-1] + (-1, 32))
    amax = np.abs(blocks).max(-1, keepdims=True)
    byte = np.maximum(np.where(amax > 0, np.frexp(amax)[1] - 1 + 127, 0) - down, 1)
    scale = np.exp2(byte - 127.0)
    codes = (blocks / scale).astype(np.float32).astype(dtype).astype(np.float64)
    return np.moveaxis((codes * scale).reshape(v.shape), -1, axis)


WIDE = False


def mx_kscale(k):
    if not WIDE:
        return np.ones(k)
    levels = np.array([10, -10, 5, -5, 0])
    a = np.random.permutation(np.resize(levels, k // 512 * 4)).reshape(k // 512, 4)
    idx = np.arange(k)
    return np.exp2(a[idx // 512, idx % 128 // 32])


BF16 = ml_dtypes.bfloat16


def bf(x):
    return np.asarray(x, np.float32).astype(BF16)


def f64(x):
    return np.asarray(x).astype(np.float64)


B, H, S, D = 1, 2, 512, 512

SOFTEMAX_DENOM = np.exp(0.0) + np.exp(np.e)


def setup_inputs():
    s = mx_kscale(D)
    return {"query": bf(np.random.standard_normal((B, H, S, D)) * s),
            "key": bf(np.random.standard_normal((B, H, S, D)) / s),
            "value": bf(np.random.standard_normal((B, H, S, D)))}


def reference(query, key, value):
    scale = D ** (-0.5)
    attn_scores = (mxq(f64(query), 3, "e4m3") @ mxq(f64(key), 3, "e4m3").transpose(0, 1, 3, 2)) * scale
    attn_weights = np.exp(attn_scores) / SOFTEMAX_DENOM
    attn_output = mxq(attn_weights, 3, "e4m3") @ mxq(f64(value), 2, "e4m3")
    return attn_output, attn_weights

@@ -1,0 +1,136 @@
+import math
+from contextlib import ExitStack
+
+import concourse.mybir as mybir
+from concourse.masks import make_identity
+
+F32 = mybir.dt.float32
+BF16 = mybir.dt.bfloat16
+U32 = mybir.dt.uint32
+U8 = mybir.dt.uint8
+FP8X4 = mybir.dt.float8_e4m3fn_x4
+EXP = mybir.ActivationFunctionType.Exp
+
+P = 128
+PACK = 4
+HEADS = 2
+S = 512
+D = 512
+NT = S // P
+FLOPS = 2 * 2 * HEADS * S * S * D
+
+SCALE = D ** (-0.5)
+NEG_LOG_C = -math.log(1.0 + math.exp(math.exp(1.0)))
+
+
+def tile_curveattention_kernel(tc, query, key, value, out_0, out_1):
+    nc = tc.nc
+    with ExitStack() as ctx:
+        keep = ctx.enter_context(tc.tile_pool(name="keep", bufs=1))
+        psum = ctx.enter_context(tc.psum_pool(name="psum", bufs=8))
+
+        ident = keep.tile([P, P], F32, name="ident")
+        make_identity(nc, ident[:])
+        warm = keep.tile([P, 1], F32, name="warm")
+        nc.vector.memset(warm[:], 0.0)
+        warm2 = keep.tile([P, 1], F32, name="warm2")
+        nc.scalar.activation(out=warm2[:], in_=warm[:], func=EXP)
+
+        raw = {}
+        for h in range(HEADS):
+            for nm, src in (("k", key), ("q", query), ("v", value)):
+                t = keep.tile([P, NT * D], BF16, name="raw_%s%d" % (nm, h))
+                nc.sync.dma_start(out=t[:], in_=src[0, h].rearrange("(p t) d -> p (t d)", t=NT))
+                raw[(nm, h)] = t
+
+        grouped = {}
+        codes = {}
+        scales = {}
+        for h in range(HEADS):
+            for nm in ("k", "q", "v", "w"):
+                grouped[(nm, h)] = keep.tile([P, PACK * S], BF16, name="grp_%s%d" % (nm, h), align_bytes=64)
+                codes[(nm, h)] = keep.tile([P, S], U32, name="cod_%s%d" % (nm, h), align_bytes=64)
+                scales[(nm, h)] = keep.tile([P, S], U8, name="scl_%s%d" % (nm, h), align_bytes=64)
+
+        def quantise(nm, h, c0, c1):
+            nc.vector.quantize_mx(
+                out=codes[(nm, h)][:, c0:c1].bitcast(FP8X4),
+                scales=scales[(nm, h)][:, c0:c1],
+                in_=grouped[(nm, h)][:, PACK * c0:PACK * c1],
+            )
+
+        def flip(nm, h):
+            words = raw[(nm, h)][:].bitcast(F32)
+            g32 = grouped[(nm, h)][:].bitcast(F32)
+            for b in range(2):
+                xt = psum.tile([P, 512], F32, name="xt", tag="bank")
+                for tl in range(2):
+                    for u in range(2):
+                        t = 2 * b + tl
+                        nc.tensor.transpose(
+                            xt[:, (2 * tl + u) * P:(2 * tl + u + 1) * P],
+                            words[:, t * 256 + u * P:t * 256 + (u + 1) * P],
+                            ident[:],
+                        )
+                dst = g32[:, b * 512:(b + 1) * 512].rearrange("p (tl c u) -> p tl c u", tl=2, u=2)
+                src = xt[:].rearrange("p (tl u c) -> p tl c u", tl=2, u=2)
+                if b == 0:
+                    nc.vector.tensor_copy(out=dst, in_=src)
+                else:
+                    nc.scalar.copy(out=dst, in_=src)
+
+        def prep_v(h):
+            dst = grouped[("v", h)][:].rearrange("p (c i t) -> p c t i", i=4, t=PACK)
+            src = raw[("v", h)][:].rearrange("p (t c i) -> p c t i", i=4, t=PACK)
+            nc.vector.tensor_copy(out=dst, in_=src)
+            quantise("v", h, 0, S)
+
+        w_out = {}
+        o_out = {}
+        for h in range(HEADS):
+            w_out[h] = keep.tile([P, NT, S], F32, name="w_out%d" % h)
+            o_out[h] = keep.tile([P, NT, D], F32, name="o_out%d" % h)
+
+        def mx(out, a, ha, a0, b, hb, b0, b1):
+            nc.tensor.matmul_mx(
+                out=out,
+                lhsT=codes[(a, ha)][:, a0:a0 + P].bitcast(FP8X4),
+                lhsT_scale=scales[(a, ha)][:, a0:a0 + P],
+                rhs=codes[(b, hb)][:, b0:b1].bitcast(FP8X4),
+                rhs_scale=scales[(b, hb)][:, b0:b1],
+                start=True,
+                stop=True,
+            )
+
+        def main(h, tq):
+            q0 = tq * P
+            st = psum.tile([P, 512], F32, name="st", tag="bank")
+            for t in range(NT):
+                mx(st[:, t * P:(t + 1) * P], "k", h, t * P, "q", h, q0, q0 + P)
+            s = psum.tile([P, 512], F32, name="s", tag="bank")
+            mx(s[:], "q", h, q0, "k", h, 0, S)
+            nc.scalar.activation(
+                out=grouped[("w", h)][:, PACK * q0:PACK * (q0 + P)].rearrange("p (c t) -> p c t", t=PACK),
+                in_=st[:].rearrange("p (t c) -> p c t", t=PACK),
+                func=EXP, scale=SCALE, bias=NEG_LOG_C,
+            )
+            nc.scalar.activation(
+                out=w_out[h][:, tq, :].rearrange("p (c t) -> p c t", t=NT),
+                in_=s[:].rearrange("p (t c) -> p c t", t=NT),
+                func=EXP, scale=SCALE, bias=NEG_LOG_C,
+            )
+            nc.sync.dma_start(out=out_1[0, h].rearrange("(p t) k -> p t k", t=NT)[:, tq, :], in_=w_out[h][:, tq, :])
+            quantise("w", h, q0, q0 + P)
+            o = psum.tile([P, 512], F32, name="o", tag="bank")
+            mx(o[:], "w", h, q0, "v", h, 0, D)
+            nc.vector.tensor_copy(out=o_out[h][:, tq, :], in_=o[:])
+            nc.sync.dma_start(out=out_0[0, h].rearrange("(p t) d -> p t d", t=NT)[:, tq, :], in_=o_out[h][:, tq, :])
+
+        for h in range(HEADS):
+            flip("k", h)
+            flip("q", h)
+            quantise("k", h, 0, S)
+            quantise("q", h, 0, S)
+            prep_v(h)
+            for tq in range(NT):
+                main(h, tq)

@@ -22,12 +22,36 @@ FLOPS = 2 * 2 * HEADS * S * S * D
 SCALE = D ** (-0.5)
 NEG_LOG_C = -math.log(1.0 + math.exp(math.exp(1.0)))
 
+ORDER = (
+    ("T", "k", 0, 0), ("Ea", "k", 0, 0), ("T", "k", 0, 1), ("Ev", "k", 0, 1), ("T", "q", 0, 0),
+    ("Ea", "q", 0, 0), ("Q", "k", 0, 0), ("T", "q", 0, 1), ("Q", "k", 0, 1), ("Ea", "q", 0, 1),
+    ("Q", "q", 0, 0), ("VR", "v", 0, 0), ("ST", "", 0, 0), ("S", "", 0, 0), ("XST", "", 0, 0),
+    ("S", "", 1, 0), ("ST", "", 1, 0), ("Q", "q", 0, 1), ("XS", "", 0, 0), ("T", "k", 1, 0),
+    ("Q", "v", 0, 2), ("XS", "", 1, 0), ("T", "k", 1, 1), ("QW", "w", 0, 0), ("SW", "", 0, 0),
+    ("Ev", "k", 1, 0), ("T", "q", 1, 0), ("XST", "", 1, 0), ("SW", "", 1, 0), ("O", "", 0, 0),
+    ("Ev", "k", 1, 1), ("Ea", "q", 1, 0), ("S", "", 2, 0), ("QW", "w", 1, 0), ("ST", "", 2, 0),
+    ("EOa", "o", 0, 0), ("Q", "k", 1, 0), ("S", "", 3, 0), ("Q", "k", 1, 1), ("O", "", 1, 0),
+    ("XS", "", 2, 0), ("Q", "q", 1, 0), ("SO", "", 0, 0), ("ST", "", 3, 0), ("EOv", "o", 1, 0),
+    ("T", "q", 1, 1), ("XST", "", 2, 0), ("SW", "", 2, 0), ("VR", "v", 1, 0), ("S", "", 4, 0),
+    ("XS", "", 3, 0), ("SO", "", 1, 0), ("ST", "", 4, 0), ("S", "", 5, 0), ("XST", "", 3, 0),
+    ("SW", "", 3, 0), ("ST", "", 5, 0), ("QW", "w", 2, 0), ("Q", "v", 1, 2), ("XS", "", 4, 0),
+    ("O", "", 2, 0), ("QW", "w", 3, 0), ("EOa", "o", 2, 0), ("Ev", "q", 1, 1), ("SW", "", 4, 0),
+    ("O", "", 3, 0), ("XST", "", 4, 0), ("SO", "", 2, 0), ("Q", "q", 1, 1), ("EOv", "o", 3, 0),
+    ("XS", "", 5, 0), ("S", "", 6, 0), ("QW", "w", 4, 0), ("ST", "", 6, 0), ("SO", "", 3, 0),
+    ("XST", "", 5, 0), ("ST", "", 7, 0), ("SW", "", 5, 0), ("O", "", 4, 0), ("XS", "", 6, 0),
+    ("QW", "w", 5, 0), ("S", "", 7, 0), ("EOv", "o", 4, 0), ("O", "", 5, 0), ("XST", "", 6, 0),
+    ("SW", "", 6, 0), ("EOv", "o", 5, 0), ("XST", "", 7, 0), ("SO", "", 4, 0), ("QW", "w", 6, 0),
+    ("XS", "", 7, 0), ("SO", "", 5, 0), ("QW", "w", 7, 0), ("O", "", 6, 0), ("O", "", 7, 0),
+    ("EOa", "o", 6, 0), ("SW", "", 7, 0), ("EOv", "o", 7, 0), ("SO", "", 6, 0), ("SO", "", 7, 0),
+)
+
 
 def tile_curveattention_kernel(tc, query, key, value, out_0, out_1):
     nc = tc.nc
     with ExitStack() as ctx:
         keep = ctx.enter_context(tc.tile_pool(name="keep", bufs=1))
         psum = ctx.enter_context(tc.psum_pool(name="psum", bufs=8))
+        ctx.enter_context(tc.manual_schedule())
 
         ident = keep.tile([P, P], F32, name="ident")
         make_identity(nc, ident[:])
@@ -36,21 +60,35 @@ def tile_curveattention_kernel(tc, query, key, value, out_0, out_1):
         warm2 = keep.tile([P, 1], F32, name="warm2")
         nc.scalar.activation(out=warm2[:], in_=warm[:], func=EXP)
 
+        srcs = {"k": key, "q": query, "v": value}
         raw = {}
-        for h in range(HEADS):
-            for nm, src in (("k", key), ("q", query), ("v", value)):
-                t = keep.tile([P, NT * D], BF16, name="raw_%s%d" % (nm, h))
-                nc.sync.dma_start(out=t[:], in_=src[0, h].rearrange("(p t) d -> p (t d)", t=NT))
-                raw[(nm, h)] = t
-
         grouped = {}
         codes = {}
         scales = {}
+        w_out = {}
+        o_out = {}
         for h in range(HEADS):
+            for nm in ("k", "q", "v"):
+                raw[(nm, h)] = keep.tile([P, NT * D], BF16, name="raw_%s%d" % (nm, h))
             for nm in ("k", "q", "v", "w"):
                 grouped[(nm, h)] = keep.tile([P, PACK * S], BF16, name="grp_%s%d" % (nm, h), align_bytes=64)
                 codes[(nm, h)] = keep.tile([P, S], U32, name="cod_%s%d" % (nm, h), align_bytes=64)
                 scales[(nm, h)] = keep.tile([P, S], U8, name="scl_%s%d" % (nm, h), align_bytes=64)
+            w_out[h] = keep.tile([P, NT, S], F32, name="w_out%d" % h)
+            o_out[h] = keep.tile([P, NT, D], F32, name="o_out%d" % h)
+
+        def load(nm, h, c0, c1):
+            nc.sync.dma_start(
+                out=raw[(nm, h)][:, c0:c1],
+                in_=srcs[nm][0, h].rearrange("(p t) d -> p (t d)", t=NT)[:, c0:c1],
+            )
+
+        for nm, h, halves in (("k", 0, 2), ("q", 0, 2), ("v", 0, 1), ("k", 1, 1), ("q", 1, 1), ("v", 1, 1)):
+            w = NT * D // halves
+            for i in range(halves):
+                load(nm, h, i * w, (i + 1) * w)
+
+        banks = {}
 
         def quantise(nm, h, c0, c1):
             nc.vector.quantize_mx(
@@ -59,78 +97,96 @@ def tile_curveattention_kernel(tc, query, key, value, out_0, out_1):
                 in_=grouped[(nm, h)][:, PACK * c0:PACK * c1],
             )
 
-        def flip(nm, h):
+        def flip(nm, h, b):
             words = raw[(nm, h)][:].bitcast(F32)
-            g32 = grouped[(nm, h)][:].bitcast(F32)
-            for b in range(2):
-                xt = psum.tile([P, 512], F32, name="xt", tag="bank")
-                for tl in range(2):
-                    for u in range(2):
-                        t = 2 * b + tl
-                        nc.tensor.transpose(
-                            xt[:, (2 * tl + u) * P:(2 * tl + u + 1) * P],
-                            words[:, t * 256 + u * P:t * 256 + (u + 1) * P],
-                            ident[:],
-                        )
-                dst = g32[:, b * 512:(b + 1) * 512].rearrange("p (tl c u) -> p tl c u", tl=2, u=2)
-                src = xt[:].rearrange("p (tl u c) -> p tl c u", tl=2, u=2)
-                if b == 0:
-                    nc.vector.tensor_copy(out=dst, in_=src)
-                else:
-                    nc.scalar.copy(out=dst, in_=src)
+            xt = psum.tile([P, 512], F32, name="xt", tag="bank")
+            banks[("T", nm, h, b)] = xt
+            for tl in range(2):
+                for u in range(2):
+                    t = 2 * b + tl
+                    nc.tensor.transpose(
+                        xt[:, (2 * tl + u) * P:(2 * tl + u + 1) * P],
+                        words[:, t * 256 + u * P:t * 256 + (u + 1) * P],
+                        ident[:],
+                    )
 
-        def prep_v(h):
+        def flip_out(nm, h, b, eng):
+            g32 = grouped[(nm, h)][:].bitcast(F32)
+            xt = banks[("T", nm, h, b)]
+            dst = g32[:, b * 512:(b + 1) * 512].rearrange("p (tl c u) -> p tl c u", tl=2, u=2)
+            src = xt[:].rearrange("p (tl u c) -> p tl c u", tl=2, u=2)
+            if eng == "v":
+                nc.vector.tensor_copy(out=dst, in_=src)
+            else:
+                nc.scalar.copy(out=dst, in_=src)
+
+        def regroup_v(h):
             dst = grouped[("v", h)][:].rearrange("p (c i t) -> p c t i", i=4, t=PACK)
             src = raw[("v", h)][:].rearrange("p (t c i) -> p c t i", i=4, t=PACK)
             nc.vector.tensor_copy(out=dst, in_=src)
-            quantise("v", h, 0, S)
 
-        w_out = {}
-        o_out = {}
-        for h in range(HEADS):
-            w_out[h] = keep.tile([P, NT, S], F32, name="w_out%d" % h)
-            o_out[h] = keep.tile([P, NT, D], F32, name="o_out%d" % h)
-
-        def mx(out, a, ha, a0, b, hb, b0, b1):
+        def mx(out, a, b, h, a0, b0, b1):
             nc.tensor.matmul_mx(
                 out=out,
-                lhsT=codes[(a, ha)][:, a0:a0 + P].bitcast(FP8X4),
-                lhsT_scale=scales[(a, ha)][:, a0:a0 + P],
-                rhs=codes[(b, hb)][:, b0:b1].bitcast(FP8X4),
-                rhs_scale=scales[(b, hb)][:, b0:b1],
+                lhsT=codes[(a, h)][:, a0:a0 + P].bitcast(FP8X4),
+                lhsT_scale=scales[(a, h)][:, a0:a0 + P],
+                rhs=codes[(b, h)][:, b0:b1].bitcast(FP8X4),
+                rhs_scale=scales[(b, h)][:, b0:b1],
                 start=True,
                 stop=True,
             )
 
-        def main(h, tq):
+        def step(kind, nm, i, b):
+            h, tq = i // NT, i % NT
             q0 = tq * P
-            st = psum.tile([P, 512], F32, name="st", tag="bank")
-            for t in range(NT):
-                mx(st[:, t * P:(t + 1) * P], "k", h, t * P, "q", h, q0, q0 + P)
-            s = psum.tile([P, 512], F32, name="s", tag="bank")
-            mx(s[:], "q", h, q0, "k", h, 0, S)
-            nc.scalar.activation(
-                out=grouped[("w", h)][:, PACK * q0:PACK * (q0 + P)].rearrange("p (c t) -> p c t", t=PACK),
-                in_=st[:].rearrange("p (t c) -> p c t", t=PACK),
-                func=EXP, scale=SCALE, bias=NEG_LOG_C,
-            )
-            nc.scalar.activation(
-                out=w_out[h][:, tq, :].rearrange("p (c t) -> p c t", t=NT),
-                in_=s[:].rearrange("p (t c) -> p c t", t=NT),
-                func=EXP, scale=SCALE, bias=NEG_LOG_C,
-            )
-            nc.sync.dma_start(out=out_1[0, h].rearrange("(p t) k -> p t k", t=NT)[:, tq, :], in_=w_out[h][:, tq, :])
-            quantise("w", h, q0, q0 + P)
-            o = psum.tile([P, 512], F32, name="o", tag="bank")
-            mx(o[:], "w", h, q0, "v", h, 0, D)
-            nc.vector.tensor_copy(out=o_out[h][:, tq, :], in_=o[:])
-            nc.sync.dma_start(out=out_0[0, h].rearrange("(p t) d -> p t d", t=NT)[:, tq, :], in_=o_out[h][:, tq, :])
+            if kind == "T":
+                flip(nm, i, b)
+            elif kind == "Ea" or kind == "Ev":
+                flip_out(nm, i, b, kind[1])
+            elif kind == "VR":
+                regroup_v(i)
+            elif kind == "QW":
+                quantise("w", h, q0, q0 + P)
+            elif kind == "Q":
+                if b == 2:
+                    quantise(nm, i, 0, S)
+                else:
+                    quantise(nm, i, b * 256, (b + 1) * 256)
+            elif kind == "ST":
+                st = psum.tile([P, 512], F32, name="st", tag="bank")
+                banks[("ST", i)] = st
+                for t in range(NT):
+                    mx(st[:, t * P:(t + 1) * P], "k", "q", h, t * P, q0, q0 + P)
+            elif kind == "SW":
+                nc.sync.dma_start(out=out_1[0, h].rearrange("(p t) k -> p t k", t=NT)[:, tq, :], in_=w_out[h][:, tq, :])
+            elif kind == "SO":
+                nc.sync.dma_start(out=out_0[0, h].rearrange("(p t) d -> p t d", t=NT)[:, tq, :], in_=o_out[h][:, tq, :])
+            elif kind == "S":
+                s = psum.tile([P, 512], F32, name="s", tag="bank")
+                banks[("S", i)] = s
+                mx(s[:], "q", "k", h, q0, 0, S)
+            elif kind == "XST":
+                nc.scalar.activation(
+                    out=grouped[("w", h)][:, PACK * q0:PACK * (q0 + P)].rearrange("p (c t) -> p c t", t=PACK),
+                    in_=banks[("ST", i)][:].rearrange("p (t c) -> p c t", t=PACK),
+                    func=EXP, scale=SCALE, bias=NEG_LOG_C,
+                )
+            elif kind == "XS":
+                nc.scalar.activation(
+                    out=w_out[h][:, tq, :].rearrange("p (c t) -> p c t", t=NT),
+                    in_=banks[("S", i)][:].rearrange("p (t c) -> p c t", t=NT),
+                    func=EXP, scale=SCALE, bias=NEG_LOG_C,
+                )
+            elif kind == "EOv":
+                nc.vector.tensor_copy(out=o_out[h][:, tq, :], in_=banks[("O", i)][:])
+            elif kind == "EOa":
+                nc.scalar.copy(out=o_out[h][:, tq, :], in_=banks[("O", i)][:])
+            elif kind == "O":
+                o = psum.tile([P, 512], F32, name="o", tag="bank")
+                banks[("O", i)] = o
+                mx(o[:], "w", "v", h, q0, 0, D)
+            else:
+                assert False, kind
 
-        for h in range(HEADS):
-            flip("k", h)
-            flip("q", h)
-            quantise("k", h, 0, S)
-            quantise("q", h, 0, S)
-            prep_v(h)
-            for tq in range(NT):
-                main(h, tq)
+        for kind, nm, i, b in ORDER:
+            step(kind, nm, i, b)

@@ -22,27 +22,36 @@ FLOPS = 2 * 2 * HEADS * S * S * D
 SCALE = D ** (-0.5)
 NEG_LOG_C = -math.log(1.0 + math.exp(math.exp(1.0)))
 
+LOADS = (("q", 0, 0, 1), ("k", 0, 0, 2), ("k", 0, 2, 1), ("k", 0, 3, 1), ("q", 0, 1, 1), ("q", 0, 2, 2), ("v", 0, 0, 4), ("k", 1, 0, 4), ("q", 1, 0, 4), ("v", 1, 0, 4))
+
 ORDER = (
-    ("T", "k", 0, 0), ("Ea", "k", 0, 0), ("T", "k", 0, 1), ("Ev", "k", 0, 1), ("T", "q", 0, 0),
-    ("Ea", "q", 0, 0), ("Q", "k", 0, 0), ("T", "q", 0, 1), ("Q", "k", 0, 1), ("Ea", "q", 0, 1),
-    ("Q", "q", 0, 0), ("VR", "v", 0, 0), ("ST", "", 0, 0), ("S", "", 0, 0), ("XST", "", 0, 0),
-    ("S", "", 1, 0), ("ST", "", 1, 0), ("Q", "q", 0, 1), ("XS", "", 0, 0), ("T", "k", 1, 0),
-    ("Q", "v", 0, 2), ("XS", "", 1, 0), ("T", "k", 1, 1), ("QW", "w", 0, 0), ("SW", "", 0, 0),
-    ("Ev", "k", 1, 0), ("T", "q", 1, 0), ("XST", "", 1, 0), ("SW", "", 1, 0), ("O", "", 0, 0),
-    ("Ev", "k", 1, 1), ("Ea", "q", 1, 0), ("S", "", 2, 0), ("QW", "w", 1, 0), ("ST", "", 2, 0),
-    ("EOa", "o", 0, 0), ("Q", "k", 1, 0), ("S", "", 3, 0), ("Q", "k", 1, 1), ("O", "", 1, 0),
-    ("XS", "", 2, 0), ("Q", "q", 1, 0), ("SO", "", 0, 0), ("ST", "", 3, 0), ("EOv", "o", 1, 0),
-    ("T", "q", 1, 1), ("XST", "", 2, 0), ("SW", "", 2, 0), ("VR", "v", 1, 0), ("S", "", 4, 0),
-    ("XS", "", 3, 0), ("SO", "", 1, 0), ("ST", "", 4, 0), ("S", "", 5, 0), ("XST", "", 3, 0),
-    ("SW", "", 3, 0), ("ST", "", 5, 0), ("QW", "w", 2, 0), ("Q", "v", 1, 2), ("XS", "", 4, 0),
-    ("O", "", 2, 0), ("QW", "w", 3, 0), ("EOa", "o", 2, 0), ("Ev", "q", 1, 1), ("SW", "", 4, 0),
-    ("O", "", 3, 0), ("XST", "", 4, 0), ("SO", "", 2, 0), ("Q", "q", 1, 1), ("EOv", "o", 3, 0),
-    ("XS", "", 5, 0), ("S", "", 6, 0), ("QW", "w", 4, 0), ("ST", "", 6, 0), ("SO", "", 3, 0),
-    ("XST", "", 5, 0), ("ST", "", 7, 0), ("SW", "", 5, 0), ("O", "", 4, 0), ("XS", "", 6, 0),
-    ("QW", "w", 5, 0), ("S", "", 7, 0), ("EOv", "o", 4, 0), ("O", "", 5, 0), ("XST", "", 6, 0),
-    ("SW", "", 6, 0), ("EOv", "o", 5, 0), ("XST", "", 7, 0), ("SO", "", 4, 0), ("QW", "w", 6, 0),
-    ("XS", "", 7, 0), ("SO", "", 5, 0), ("QW", "w", 7, 0), ("O", "", 6, 0), ("O", "", 7, 0),
-    ("EOa", "o", 6, 0), ("SW", "", 7, 0), ("EOv", "o", 7, 0), ("SO", "", 6, 0), ("SO", "", 7, 0),
+    ("T", "q", 0, 0, 1), ("Ea", "q", 0, 0, 1), ("T", "k", 0, 0, 2), ("Q", "q", 0, 0, 1),
+    ("T", "k", 0, 2, 1), ("Ev", "k", 0, 0, 2), ("T", "k", 0, 3, 1), ("Ea", "k", 0, 2, 1),
+    ("T", "q", 0, 1, 1), ("Ea", "k", 0, 3, 1), ("Q", "k", 0, 0, 2), ("T", "q", 0, 2, 2),
+    ("Ea", "q", 0, 1, 1), ("Q", "k", 0, 2, 1), ("Q", "k", 0, 3, 1), ("Q", "q", 0, 1, 1),
+    ("Ea", "q", 0, 2, 2), ("S", "", 0, 0, 0), ("VR", "v", 0, 0, 0), ("ST", "", 0, 0, 0),
+    ("XS", "", 0, 0, 0), ("S", "", 1, 0, 0), ("ST", "", 1, 0, 0), ("Q", "q", 0, 2, 2),
+    ("XS", "", 1, 0, 0), ("T", "k", 1, 2, 2), ("Q", "v", 0, 0, 4), ("XST", "", 0, 0, 0),
+    ("T", "k", 1, 0, 2), ("Ev", "k", 1, 2, 2), ("SW", "", 0, 0, 0), ("XST", "", 1, 0, 0),
+    ("T", "q", 1, 0, 2), ("SW", "", 1, 0, 0), ("QW", "", 0, 0, 0), ("Q", "k", 1, 2, 2),
+    ("Ea", "k", 1, 0, 2), ("QW", "", 1, 0, 0), ("S", "", 2, 0, 0), ("Ev", "q", 1, 0, 2),
+    ("S", "", 3, 0, 0), ("XS", "", 2, 0, 0), ("O", "", 0, 0, 0), ("Q", "k", 1, 0, 2),
+    ("ST", "", 2, 0, 0), ("XS", "", 3, 0, 0), ("Q", "q", 1, 0, 2), ("SW", "", 2, 0, 0),
+    ("O", "", 1, 0, 0), ("EOv", "", 0, 0, 512), ("ST", "", 3, 0, 0), ("XST", "", 2, 0, 0),
+    ("T", "q", 1, 2, 2), ("SW", "", 3, 0, 0), ("EOv", "", 1, 0, 512), ("XST", "", 3, 0, 0),
+    ("SO", "", 0, 0, 512), ("S", "", 4, 0, 0), ("QW", "", 2, 0, 0), ("Ev", "q", 1, 2, 2),
+    ("S", "", 5, 0, 0), ("XS", "", 4, 0, 0), ("SO", "", 1, 0, 512), ("ST", "", 4, 0, 0),
+    ("QW", "", 3, 0, 0), ("O", "", 2, 0, 0), ("Q", "q", 1, 2, 2), ("XS", "", 5, 0, 0),
+    ("SW", "", 4, 0, 0), ("VR", "v", 1, 0, 0), ("O", "", 3, 0, 0), ("XST", "", 4, 0, 0),
+    ("S", "", 6, 0, 0), ("SW", "", 5, 0, 0), ("ST", "", 5, 0, 0), ("XS", "", 6, 0, 0),
+    ("S", "", 7, 0, 0), ("EOv", "", 2, 0, 512), ("ST", "", 6, 0, 0), ("XST", "", 5, 0, 0),
+    ("ST", "", 7, 0, 0), ("EOv", "", 3, 0, 512), ("SO", "", 2, 0, 512), ("XS", "", 7, 0, 0),
+    ("QW", "", 4, 0, 0), ("SO", "", 3, 0, 512), ("Q", "v", 1, 0, 4), ("XST", "", 6, 0, 0),
+    ("SW", "", 6, 0, 0), ("QW", "", 5, 0, 0), ("O", "", 4, 0, 0), ("XST", "", 7, 0, 0),
+    ("SW", "", 7, 0, 0), ("QW", "", 6, 0, 0), ("O", "", 5, 0, 0), ("EOv", "", 4, 0, 512),
+    ("O", "", 6, 0, 0), ("EOa", "", 5, 0, 512), ("QW", "", 7, 0, 0), ("SO", "", 4, 0, 512),
+    ("EOv", "", 6, 0, 512), ("O", "", 7, 0, 0), ("SO", "", 5, 0, 512), ("EOv", "", 7, 0, 256),
+    ("SO", "", 6, 0, 512), ("EOv", "", 7, 256, 256), ("SO", "", 7, 0, 256), ("SO", "", 7, 256, 256),
 )
 
 
@@ -77,16 +86,11 @@ def tile_curveattention_kernel(tc, query, key, value, out_0, out_1):
             w_out[h] = keep.tile([P, NT, S], F32, name="w_out%d" % h)
             o_out[h] = keep.tile([P, NT, D], F32, name="o_out%d" % h)
 
-        def load(nm, h, c0, c1):
+        for nm, h, t0, nt in LOADS:
             nc.sync.dma_start(
-                out=raw[(nm, h)][:, c0:c1],
-                in_=srcs[nm][0, h].rearrange("(p t) d -> p (t d)", t=NT)[:, c0:c1],
+                out=raw[(nm, h)][:, t0 * D:(t0 + nt) * D],
+                in_=srcs[nm][0, h].rearrange("(p t) d -> p (t d)", t=NT)[:, t0 * D:(t0 + nt) * D],
             )
-
-        for nm, h, halves in (("k", 0, 2), ("q", 0, 2), ("v", 0, 1), ("k", 1, 1), ("q", 1, 1), ("v", 1, 1)):
-            w = NT * D // halves
-            for i in range(halves):
-                load(nm, h, i * w, (i + 1) * w)
 
         banks = {}
 
@@ -97,24 +101,23 @@ def tile_curveattention_kernel(tc, query, key, value, out_0, out_1):
                 in_=grouped[(nm, h)][:, PACK * c0:PACK * c1],
             )
 
-        def flip(nm, h, b):
+        def flip(nm, h, t0, nt):
             words = raw[(nm, h)][:].bitcast(F32)
-            xt = psum.tile([P, 512], F32, name="xt", tag="bank")
-            banks[("T", nm, h, b)] = xt
-            for tl in range(2):
+            xt = psum.tile([P, nt * 256], F32, name="xt", tag="bank")
+            banks[("T", nm, h, t0)] = xt
+            for tl in range(nt):
                 for u in range(2):
-                    t = 2 * b + tl
                     nc.tensor.transpose(
                         xt[:, (2 * tl + u) * P:(2 * tl + u + 1) * P],
-                        words[:, t * 256 + u * P:t * 256 + (u + 1) * P],
+                        words[:, (t0 + tl) * 256 + u * P:(t0 + tl) * 256 + (u + 1) * P],
                         ident[:],
                     )
 
-        def flip_out(nm, h, b, eng):
+        def flip_out(nm, h, t0, nt, eng):
             g32 = grouped[(nm, h)][:].bitcast(F32)
-            xt = banks[("T", nm, h, b)]
-            dst = g32[:, b * 512:(b + 1) * 512].rearrange("p (tl c u) -> p tl c u", tl=2, u=2)
-            src = xt[:].rearrange("p (tl u c) -> p tl c u", tl=2, u=2)
+            xt = banks[("T", nm, h, t0)]
+            dst = g32[:, t0 * 256:(t0 + nt) * 256].rearrange("p (tl c u) -> p tl c u", tl=nt, u=2)
+            src = xt[:].rearrange("p (tl u c) -> p tl c u", tl=nt, u=2)
             if eng == "v":
                 nc.vector.tensor_copy(out=dst, in_=src)
             else:
@@ -136,22 +139,19 @@ def tile_curveattention_kernel(tc, query, key, value, out_0, out_1):
                 stop=True,
             )
 
-        def step(kind, nm, i, b):
+        def step(kind, nm, i, a, b):
             h, tq = i // NT, i % NT
             q0 = tq * P
             if kind == "T":
-                flip(nm, i, b)
+                flip(nm, i, a, b)
             elif kind == "Ea" or kind == "Ev":
-                flip_out(nm, i, b, kind[1])
+                flip_out(nm, i, a, b, kind[1])
             elif kind == "VR":
                 regroup_v(i)
             elif kind == "QW":
                 quantise("w", h, q0, q0 + P)
             elif kind == "Q":
-                if b == 2:
-                    quantise(nm, i, 0, S)
-                else:
-                    quantise(nm, i, b * 256, (b + 1) * 256)
+                quantise(nm, i, a * P, (a + b) * P)
             elif kind == "ST":
                 st = psum.tile([P, 512], F32, name="st", tag="bank")
                 banks[("ST", i)] = st
@@ -160,7 +160,10 @@ def tile_curveattention_kernel(tc, query, key, value, out_0, out_1):
             elif kind == "SW":
                 nc.sync.dma_start(out=out_1[0, h].rearrange("(p t) k -> p t k", t=NT)[:, tq, :], in_=w_out[h][:, tq, :])
             elif kind == "SO":
-                nc.sync.dma_start(out=out_0[0, h].rearrange("(p t) d -> p t d", t=NT)[:, tq, :], in_=o_out[h][:, tq, :])
+                nc.sync.dma_start(
+                    out=out_0[0, h].rearrange("(p t) d -> p t d", t=NT)[:, tq, a:a + b],
+                    in_=o_out[h][:, tq, a:a + b],
+                )
             elif kind == "S":
                 s = psum.tile([P, 512], F32, name="s", tag="bank")
                 banks[("S", i)] = s
@@ -178,9 +181,9 @@ def tile_curveattention_kernel(tc, query, key, value, out_0, out_1):
                     func=EXP, scale=SCALE, bias=NEG_LOG_C,
                 )
             elif kind == "EOv":
-                nc.vector.tensor_copy(out=o_out[h][:, tq, :], in_=banks[("O", i)][:])
+                nc.vector.tensor_copy(out=o_out[h][:, tq, a:a + b], in_=banks[("O", i)][:, a:a + b])
             elif kind == "EOa":
-                nc.scalar.copy(out=o_out[h][:, tq, :], in_=banks[("O", i)][:])
+                nc.scalar.copy(out=o_out[h][:, tq, a:a + b], in_=banks[("O", i)][:, a:a + b])
             elif kind == "O":
                 o = psum.tile([P, 512], F32, name="o", tag="bank")
                 banks[("O", i)] = o
@@ -188,5 +191,5 @@ def tile_curveattention_kernel(tc, query, key, value, out_0, out_1):
             else:
                 assert False, kind
 
-        for kind, nm, i, b in ORDER:
-            step(kind, nm, i, b)
+        for kind, nm, i, a, b in ORDER:
+            step(kind, nm, i, a, b)

@@ -10,6 +10,8 @@ U32 = mybir.dt.uint32
 U8 = mybir.dt.uint8
 FP8X4 = mybir.dt.float8_e4m3fn_x4
 EXP = mybir.ActivationFunctionType.Exp
+MULT = mybir.AluOpType.mult
+ADD = mybir.AluOpType.add
 
 P = 128
 PACK = 4
@@ -22,36 +24,38 @@ FLOPS = 2 * 2 * HEADS * S * S * D
 SCALE = D ** (-0.5)
 NEG_LOG_C = -math.log(1.0 + math.exp(math.exp(1.0)))
 
-LOADS = (("q", 0, 0, 1), ("k", 0, 0, 2), ("k", 0, 2, 1), ("k", 0, 3, 1), ("q", 0, 1, 1), ("q", 0, 2, 2), ("v", 0, 0, 4), ("k", 1, 0, 4), ("q", 1, 0, 4), ("v", 1, 0, 4))
+LOADS = (("q", 0, 0, 1), ("k", 0, 0, 2), ("k", 0, 2, 1), ("k", 0, 3, 1), ("q", 0, 1, 1), ("q", 0, 2, 2), ("k", 1, 0, 2), ("k", 1, 2, 2), ("v", 0, 0, 4), ("q", 1, 0, 4), ("v", 1, 0, 4))
 
 ORDER = (
-    ("T", "q", 0, 0, 1), ("Ea", "q", 0, 0, 1), ("T", "k", 0, 0, 2), ("Q", "q", 0, 0, 1),
-    ("T", "k", 0, 2, 1), ("Ev", "k", 0, 0, 2), ("T", "k", 0, 3, 1), ("Ea", "k", 0, 2, 1),
-    ("T", "q", 0, 1, 1), ("Ea", "k", 0, 3, 1), ("Q", "k", 0, 0, 2), ("T", "q", 0, 2, 2),
-    ("Ea", "q", 0, 1, 1), ("Q", "k", 0, 2, 1), ("Q", "k", 0, 3, 1), ("Q", "q", 0, 1, 1),
-    ("Ea", "q", 0, 2, 2), ("S", "", 0, 0, 0), ("VR", "v", 0, 0, 0), ("ST", "", 0, 0, 0),
-    ("XS", "", 0, 0, 0), ("S", "", 1, 0, 0), ("ST", "", 1, 0, 0), ("Q", "q", 0, 2, 2),
-    ("XS", "", 1, 0, 0), ("T", "k", 1, 2, 2), ("Q", "v", 0, 0, 4), ("XST", "", 0, 0, 0),
-    ("T", "k", 1, 0, 2), ("Ev", "k", 1, 2, 2), ("SW", "", 0, 0, 0), ("XST", "", 1, 0, 0),
-    ("T", "q", 1, 0, 2), ("SW", "", 1, 0, 0), ("QW", "", 0, 0, 0), ("Q", "k", 1, 2, 2),
-    ("Ea", "k", 1, 0, 2), ("QW", "", 1, 0, 0), ("S", "", 2, 0, 0), ("Ev", "q", 1, 0, 2),
-    ("S", "", 3, 0, 0), ("XS", "", 2, 0, 0), ("O", "", 0, 0, 0), ("Q", "k", 1, 0, 2),
-    ("ST", "", 2, 0, 0), ("XS", "", 3, 0, 0), ("Q", "q", 1, 0, 2), ("SW", "", 2, 0, 0),
-    ("O", "", 1, 0, 0), ("EOv", "", 0, 0, 512), ("ST", "", 3, 0, 0), ("XST", "", 2, 0, 0),
-    ("T", "q", 1, 2, 2), ("SW", "", 3, 0, 0), ("EOv", "", 1, 0, 512), ("XST", "", 3, 0, 0),
-    ("SO", "", 0, 0, 512), ("S", "", 4, 0, 0), ("QW", "", 2, 0, 0), ("Ev", "q", 1, 2, 2),
-    ("S", "", 5, 0, 0), ("XS", "", 4, 0, 0), ("SO", "", 1, 0, 512), ("ST", "", 4, 0, 0),
-    ("QW", "", 3, 0, 0), ("O", "", 2, 0, 0), ("Q", "q", 1, 2, 2), ("XS", "", 5, 0, 0),
-    ("SW", "", 4, 0, 0), ("VR", "v", 1, 0, 0), ("O", "", 3, 0, 0), ("XST", "", 4, 0, 0),
-    ("S", "", 6, 0, 0), ("SW", "", 5, 0, 0), ("ST", "", 5, 0, 0), ("XS", "", 6, 0, 0),
-    ("S", "", 7, 0, 0), ("EOv", "", 2, 0, 512), ("ST", "", 6, 0, 0), ("XST", "", 5, 0, 0),
-    ("ST", "", 7, 0, 0), ("EOv", "", 3, 0, 512), ("SO", "", 2, 0, 512), ("XS", "", 7, 0, 0),
-    ("QW", "", 4, 0, 0), ("SO", "", 3, 0, 512), ("Q", "v", 1, 0, 4), ("XST", "", 6, 0, 0),
-    ("SW", "", 6, 0, 0), ("QW", "", 5, 0, 0), ("O", "", 4, 0, 0), ("XST", "", 7, 0, 0),
-    ("SW", "", 7, 0, 0), ("QW", "", 6, 0, 0), ("O", "", 5, 0, 0), ("EOv", "", 4, 0, 512),
-    ("O", "", 6, 0, 0), ("EOa", "", 5, 0, 512), ("QW", "", 7, 0, 0), ("SO", "", 4, 0, 512),
-    ("EOv", "", 6, 0, 512), ("O", "", 7, 0, 0), ("SO", "", 5, 0, 512), ("EOv", "", 7, 0, 256),
-    ("SO", "", 6, 0, 512), ("EOv", "", 7, 256, 256), ("SO", "", 7, 0, 256), ("SO", "", 7, 256, 256),
+    ("T", "q", 0, 0, 1), ("EA", "q", 0, 0, 1), ("T", "k", 0, 0, 2), ("T", "k", 0, 2, 1),
+    ("Q", "q", 0, 0, 1), ("ED", "k", 0, 0, 2), ("T", "k", 0, 3, 1), ("EA", "k", 0, 2, 1),
+    ("T", "q", 0, 1, 1), ("EA", "k", 0, 3, 1), ("T", "q", 0, 2, 2), ("EA", "q", 0, 1, 1),
+    ("Q", "k", 0, 0, 2), ("T", "k", 1, 0, 2), ("Q", "k", 0, 2, 1), ("Q", "k", 0, 3, 1),
+    ("EA", "q", 0, 2, 2), ("Q", "q", 0, 1, 1), ("S", "", 0, 0, 0), ("ED", "k", 1, 0, 2),
+    ("S", "", 1, 0, 0), ("Q", "q", 0, 2, 2), ("XS", "", 0, 0, 0), ("T", "k", 1, 2, 2),
+    ("VP", "v", 0, 0, 1), ("S", "", 2, 0, 0), ("XS", "", 1, 0, 0), ("ED", "k", 1, 2, 2),
+    ("ST", "", 0, 0, 0), ("VP", "v", 0, 1, 1), ("SW", "", 0, 0, 1), ("XS", "", 2, 0, 0),
+    ("Q", "k", 1, 0, 2), ("T", "q", 1, 0, 2), ("SW", "", 1, 0, 1), ("VP", "v", 0, 2, 1),
+    ("Q", "k", 1, 2, 2), ("XST", "", 0, 0, 0), ("ST", "", 1, 0, 0), ("SW", "", 2, 0, 1),
+    ("ED", "q", 1, 0, 2), ("S", "", 3, 0, 0), ("VP", "v", 0, 3, 1), ("XST", "", 1, 0, 0),
+    ("ST", "", 2, 0, 0), ("QW", "", 0, 0, 1), ("T", "q", 1, 2, 2), ("Q", "v", 0, 0, 2),
+    ("VP", "v", 1, 0, 1), ("XS", "", 3, 0, 0), ("Q", "q", 1, 0, 2), ("ST", "", 3, 0, 0),
+    ("Q", "v", 0, 2, 2), ("XST", "", 2, 0, 0), ("VP", "v", 1, 1, 1), ("QW", "", 1, 0, 1),
+    ("SW", "", 3, 0, 1), ("ED", "q", 1, 2, 2), ("O", "", 0, 0, 0), ("XST", "", 3, 0, 0),
+    ("S", "", 4, 0, 0), ("VP", "v", 1, 2, 1), ("QW", "", 2, 0, 1), ("O", "", 1, 0, 0),
+    ("EOD", "", 0, 0, 512), ("XS", "", 4, 0, 0), ("S", "", 5, 0, 0), ("VP", "v", 1, 3, 1),
+    ("ST", "", 4, 0, 0), ("EOD", "", 1, 0, 512), ("XS", "", 5, 0, 0), ("O", "", 2, 0, 0),
+    ("SO", "", 0, 0, 512), ("ST", "", 5, 0, 0), ("SW", "", 4, 0, 1), ("QW", "", 3, 0, 1),
+    ("Q", "q", 1, 2, 2), ("XST", "", 4, 0, 0), ("SO", "", 1, 0, 512), ("EOD", "", 2, 0, 512),
+    ("SW", "", 5, 0, 1), ("XST", "", 5, 0, 0), ("ST", "", 6, 0, 0), ("Q", "v", 1, 0, 2),
+    ("S", "", 6, 0, 0), ("XST", "", 6, 0, 0), ("SO", "", 2, 0, 512), ("O", "", 3, 0, 0),
+    ("Q", "v", 1, 2, 2), ("ST", "", 7, 0, 0), ("QW", "", 4, 0, 1), ("EOD", "", 3, 0, 512),
+    ("S", "", 7, 0, 0), ("XST", "", 7, 0, 0), ("O", "", 4, 0, 0), ("QW", "", 5, 0, 1),
+    ("EOD", "", 4, 0, 512), ("SO", "", 3, 0, 512), ("XS", "", 6, 0, 0), ("O", "", 5, 0, 0),
+    ("QW", "", 6, 0, 1), ("XS", "", 7, 0, 0), ("QW", "", 7, 0, 1), ("SO", "", 4, 0, 512),
+    ("EOD", "", 5, 0, 512), ("SW", "", 6, 0, 1), ("O", "", 6, 0, 0), ("O", "", 7, 0, 0),
+    ("EOA", "", 6, 256, 256), ("EOD", "", 6, 0, 256), ("SO", "", 5, 0, 512), ("EOD", "", 7, 0, 512),
+    ("SW", "", 7, 0, 1), ("SO", "", 6, 0, 512), ("SO", "", 7, 0, 512),
 )
 
 
@@ -118,15 +122,20 @@ def tile_curveattention_kernel(tc, query, key, value, out_0, out_1):
             xt = banks[("T", nm, h, t0)]
             dst = g32[:, t0 * 256:(t0 + nt) * 256].rearrange("p (tl c u) -> p tl c u", tl=nt, u=2)
             src = xt[:].rearrange("p (tl u c) -> p tl c u", tl=nt, u=2)
-            if eng == "v":
+            if eng == "D":
                 nc.vector.tensor_copy(out=dst, in_=src)
             else:
                 nc.scalar.copy(out=dst, in_=src)
 
-        def regroup_v(h):
-            dst = grouped[("v", h)][:].rearrange("p (c i t) -> p c t i", i=4, t=PACK)
-            src = raw[("v", h)][:].rearrange("p (t c i) -> p c t i", i=4, t=PACK)
-            nc.vector.tensor_copy(out=dst, in_=src)
+        def regroup_v(h, c0, c1, eng):
+            if eng == "D":
+                dst = grouped[("v", h)][:, PACK * c0:PACK * c1].rearrange("p (c i t) -> p c t i", i=4, t=PACK)
+                src = raw[("v", h)][:].rearrange("p (t c i) -> p c t i", i=4, t=PACK)[:, c0 // 4:c1 // 4]
+                nc.vector.tensor_copy(out=dst, in_=src)
+            else:
+                dst = grouped[("v", h)][:, PACK * c0:PACK * c1].rearrange("p (c t) -> p c t", t=PACK)
+                src = raw[("v", h)][:].rearrange("p (t c) -> p c t", t=PACK)[:, c0:c1]
+                nc.gpsimd.tensor_scalar(out=dst, in0=src, scalar1=1.0, scalar2=0.0, op0=MULT, op1=ADD)
 
         def mx(out, a, b, h, a0, b0, b1):
             nc.tensor.matmul_mx(
@@ -144,12 +153,12 @@ def tile_curveattention_kernel(tc, query, key, value, out_0, out_1):
             q0 = tq * P
             if kind == "T":
                 flip(nm, i, a, b)
-            elif kind == "Ea" or kind == "Ev":
+            elif kind == "EA" or kind == "ED":
                 flip_out(nm, i, a, b, kind[1])
-            elif kind == "VR":
-                regroup_v(i)
+            elif kind == "VP" or kind == "VD":
+                regroup_v(i, a * P, (a + b) * P, kind[1])
             elif kind == "QW":
-                quantise("w", h, q0, q0 + P)
+                quantise("w", h, q0, q0 + b * P)
             elif kind == "Q":
                 quantise(nm, i, a * P, (a + b) * P)
             elif kind == "ST":
@@ -158,7 +167,12 @@ def tile_curveattention_kernel(tc, query, key, value, out_0, out_1):
                 for t in range(NT):
                     mx(st[:, t * P:(t + 1) * P], "k", "q", h, t * P, q0, q0 + P)
             elif kind == "SW":
-                nc.sync.dma_start(out=out_1[0, h].rearrange("(p t) k -> p t k", t=NT)[:, tq, :], in_=w_out[h][:, tq, :])
+                nc.sync.dma_start(out=out_1[0, h].rearrange("(p t) k -> p t k", t=NT)[:, tq:tq + b, :], in_=w_out[h][:, tq:tq + b, :])
+            elif kind == "SO2":
+                nc.sync.dma_start(
+                    out=out_0[0, h].rearrange("(p t) d -> p t d", t=NT)[:, tq:tq + b, :],
+                    in_=o_out[h][:, tq:tq + b, :],
+                )
             elif kind == "SO":
                 nc.sync.dma_start(
                     out=out_0[0, h].rearrange("(p t) d -> p t d", t=NT)[:, tq, a:a + b],
@@ -180,9 +194,9 @@ def tile_curveattention_kernel(tc, query, key, value, out_0, out_1):
                     in_=banks[("S", i)][:].rearrange("p (t c) -> p c t", t=NT),
                     func=EXP, scale=SCALE, bias=NEG_LOG_C,
                 )
-            elif kind == "EOv":
+            elif kind == "EOD":
                 nc.vector.tensor_copy(out=o_out[h][:, tq, a:a + b], in_=banks[("O", i)][:, a:a + b])
-            elif kind == "EOa":
+            elif kind == "EOA":
                 nc.scalar.copy(out=o_out[h][:, tq, a:a + b], in_=banks[("O", i)][:, a:a + b])
             elif kind == "O":
                 o = psum.tile([P, 512], F32, name="o", tag="bank")

@@ -31,31 +31,29 @@ ORDER = (
     ("Q", "q", 0, 0, 1), ("ED", "k", 0, 0, 2), ("T", "k", 0, 3, 1), ("EA", "k", 0, 2, 1),
     ("T", "q", 0, 1, 1), ("EA", "k", 0, 3, 1), ("T", "q", 0, 2, 2), ("EA", "q", 0, 1, 1),
     ("Q", "k", 0, 0, 2), ("T", "k", 1, 0, 2), ("Q", "k", 0, 2, 1), ("Q", "k", 0, 3, 1),
-    ("EA", "q", 0, 2, 2), ("Q", "q", 0, 1, 1), ("S", "", 0, 0, 0), ("ED", "k", 1, 0, 2),
-    ("S", "", 1, 0, 0), ("Q", "q", 0, 2, 2), ("XS", "", 0, 0, 0), ("T", "k", 1, 2, 2),
-    ("VP", "v", 0, 0, 1), ("S", "", 2, 0, 0), ("XS", "", 1, 0, 0), ("ED", "k", 1, 2, 2),
-    ("ST", "", 0, 0, 0), ("VP", "v", 0, 1, 1), ("SW", "", 0, 0, 1), ("XS", "", 2, 0, 0),
-    ("Q", "k", 1, 0, 2), ("T", "q", 1, 0, 2), ("SW", "", 1, 0, 1), ("VP", "v", 0, 2, 1),
-    ("Q", "k", 1, 2, 2), ("XST", "", 0, 0, 0), ("ST", "", 1, 0, 0), ("SW", "", 2, 0, 1),
-    ("ED", "q", 1, 0, 2), ("S", "", 3, 0, 0), ("VP", "v", 0, 3, 1), ("XST", "", 1, 0, 0),
-    ("ST", "", 2, 0, 0), ("QW", "", 0, 0, 1), ("T", "q", 1, 2, 2), ("Q", "v", 0, 0, 2),
-    ("VP", "v", 1, 0, 1), ("XS", "", 3, 0, 0), ("Q", "q", 1, 0, 2), ("ST", "", 3, 0, 0),
-    ("Q", "v", 0, 2, 2), ("XST", "", 2, 0, 0), ("VP", "v", 1, 1, 1), ("QW", "", 1, 0, 1),
-    ("SW", "", 3, 0, 1), ("ED", "q", 1, 2, 2), ("O", "", 0, 0, 0), ("XST", "", 3, 0, 0),
-    ("S", "", 4, 0, 0), ("VP", "v", 1, 2, 1), ("QW", "", 2, 0, 1), ("O", "", 1, 0, 0),
-    ("EOD", "", 0, 0, 512), ("XS", "", 4, 0, 0), ("S", "", 5, 0, 0), ("VP", "v", 1, 3, 1),
-    ("ST", "", 4, 0, 0), ("EOD", "", 1, 0, 512), ("XS", "", 5, 0, 0), ("O", "", 2, 0, 0),
-    ("SO", "", 0, 0, 512), ("ST", "", 5, 0, 0), ("SW", "", 4, 0, 1), ("QW", "", 3, 0, 1),
-    ("Q", "q", 1, 2, 2), ("XST", "", 4, 0, 0), ("SO", "", 1, 0, 512), ("EOD", "", 2, 0, 512),
-    ("SW", "", 5, 0, 1), ("XST", "", 5, 0, 0), ("ST", "", 6, 0, 0), ("Q", "v", 1, 0, 2),
-    ("S", "", 6, 0, 0), ("XST", "", 6, 0, 0), ("SO", "", 2, 0, 512), ("O", "", 3, 0, 0),
-    ("Q", "v", 1, 2, 2), ("ST", "", 7, 0, 0), ("QW", "", 4, 0, 1), ("EOD", "", 3, 0, 512),
-    ("S", "", 7, 0, 0), ("XST", "", 7, 0, 0), ("O", "", 4, 0, 0), ("QW", "", 5, 0, 1),
-    ("EOD", "", 4, 0, 512), ("SO", "", 3, 0, 512), ("XS", "", 6, 0, 0), ("O", "", 5, 0, 0),
-    ("QW", "", 6, 0, 1), ("XS", "", 7, 0, 0), ("QW", "", 7, 0, 1), ("SO", "", 4, 0, 512),
-    ("EOD", "", 5, 0, 512), ("SW", "", 6, 0, 1), ("O", "", 6, 0, 0), ("O", "", 7, 0, 0),
-    ("EOA", "", 6, 256, 256), ("EOD", "", 6, 0, 256), ("SO", "", 5, 0, 512), ("EOD", "", 7, 0, 512),
-    ("SW", "", 7, 0, 1), ("SO", "", 6, 0, 512), ("SO", "", 7, 0, 512),
+    ("EA", "q", 0, 2, 2), ("Q", "q", 0, 1, 1), ("S", "", 0, 0, 0), ("EA", "k", 1, 0, 2),
+    ("Q", "q", 0, 2, 2), ("S", "", 1, 0, 0), ("XS", "", 0, 0, 0), ("ST", "", 0, 0, 0),
+    ("Q", "k", 1, 0, 2), ("VD", "v", 0, 0, 4), ("XS", "", 1, 0, 0), ("T", "k", 1, 2, 2),
+    ("SW", "", 0, 0, 1), ("S", "", 2, 0, 0), ("XST", "", 0, 0, 0), ("ST", "", 1, 0, 0),
+    ("SW", "", 1, 0, 1), ("ED", "k", 1, 2, 2), ("XS", "", 2, 0, 0), ("T", "q", 1, 0, 2),
+    ("Q", "v", 0, 0, 4), ("S", "", 3, 0, 0), ("XST", "", 1, 0, 0), ("ST", "", 2, 0, 0),
+    ("SW", "", 2, 0, 1), ("QW", "", 0, 0, 1), ("EA", "q", 1, 0, 2), ("ST", "", 3, 0, 0),
+    ("Q", "k", 1, 2, 2), ("O", "", 0, 0, 0), ("QW", "", 1, 0, 1), ("XS", "", 3, 0, 0),
+    ("T", "q", 1, 2, 2), ("Q", "q", 1, 0, 2), ("XST", "", 2, 0, 0), ("EOD", "", 0, 0, 512),
+    ("SW", "", 3, 0, 1), ("S", "", 4, 0, 0), ("XST", "", 3, 0, 0), ("ED", "q", 1, 2, 2),
+    ("O", "", 1, 0, 0), ("ST", "", 4, 0, 0), ("SO", "", 0, 0, 512), ("XS", "", 4, 0, 0),
+    ("EOD", "", 1, 0, 512), ("S", "", 5, 0, 0), ("XST", "", 4, 0, 0), ("QW", "", 2, 0, 1),
+    ("Q", "q", 1, 2, 2), ("SW", "", 4, 0, 1), ("SO", "", 1, 0, 512), ("O", "", 2, 0, 0),
+    ("QW", "", 3, 0, 1), ("XS", "", 5, 0, 0), ("VD", "v", 1, 0, 4), ("ST", "", 5, 0, 0),
+    ("O", "", 3, 0, 0), ("XST", "", 5, 0, 0), ("S", "", 6, 0, 0), ("SW", "", 5, 0, 1),
+    ("ST", "", 6, 0, 0), ("EOD", "", 2, 0, 512), ("XS", "", 6, 0, 0), ("S", "", 7, 0, 0),
+    ("ST", "", 7, 0, 0), ("QW", "", 4, 0, 1), ("XST", "", 6, 0, 0), ("Q", "v", 1, 0, 4),
+    ("SW", "", 6, 0, 1), ("SO", "", 2, 0, 512), ("XST", "", 7, 0, 0), ("EOD", "", 3, 0, 512),
+    ("O", "", 4, 0, 0), ("XS", "", 7, 0, 0), ("QW", "", 5, 0, 1), ("QW", "", 6, 0, 1),
+    ("SO", "", 3, 0, 512), ("QW", "", 7, 0, 1), ("EOA", "", 4, 0, 512), ("O", "", 5, 0, 0),
+    ("O", "", 6, 0, 0), ("SW", "", 7, 0, 1), ("EOD", "", 5, 0, 512), ("O", "", 7, 0, 0),
+    ("EOA", "", 6, 0, 512), ("SO", "", 4, 0, 512), ("EOD", "", 7, 0, 256), ("EOA", "", 7, 256, 256),
+    ("SO", "", 5, 0, 512), ("SO", "", 6, 0, 512), ("SO", "", 7, 0, 512),
 )
 
 

@@ -61,13 +61,16 @@ def tile_curveattention_kernel(tc, query, key, value, out_0, out_1):
     nc = tc.nc
     with ExitStack() as ctx:
         keep = ctx.enter_context(tc.tile_pool(name="keep", bufs=1))
-        psum = ctx.enter_context(tc.psum_pool(name="psum", bufs=8))
+        psum = ctx.enter_context(tc.psum_pool(name="psum", bufs=7))
+        busy = ctx.enter_context(tc.psum_pool(name="busy", bufs=1))
         ctx.enter_context(tc.manual_schedule())
 
         ident = keep.tile([P, P], F32, name="ident")
         make_identity(nc, ident[:])
         warm = keep.tile([P, 1], F32, name="warm")
         nc.vector.memset(warm[:], 0.0)
+        zeros = keep.tile([P, P], F32, name="zeros")
+        nc.vector.memset(zeros[:], 0.0)
         warm2 = keep.tile([P, 1], F32, name="warm2")
         nc.scalar.activation(out=warm2[:], in_=warm[:], func=EXP)
 
@@ -146,11 +149,21 @@ def tile_curveattention_kernel(tc, query, key, value, out_0, out_1):
                 stop=True,
             )
 
+        idle_bank = busy.tile([P, 512], F32, name="idle_bank")
+
+        def keep_clock(n):
+            nc.tensor.matmul(idle_bank[:, :n], lhsT=zeros[:], rhs=zeros[:, :n], start=True, stop=True)
+
+        for i in range(4):
+            keep_clock(P)
+
         def step(kind, nm, i, a, b):
             h, tq = i // NT, i % NT
             q0 = tq * P
             if kind == "T":
                 flip(nm, i, a, b)
+                if i == 0:
+                    keep_clock(64)
             elif kind == "EA" or kind == "ED":
                 flip_out(nm, i, a, b, kind[1])
             elif kind == "VP" or kind == "VD":

@@ -27,33 +27,35 @@ NEG_LOG_C = -math.log(1.0 + math.exp(math.exp(1.0)))
 LOADS = (("q", 0, 0, 1), ("k", 0, 0, 2), ("k", 0, 2, 1), ("k", 0, 3, 1), ("q", 0, 1, 1), ("q", 0, 2, 2), ("k", 1, 0, 2), ("k", 1, 2, 2), ("v", 0, 0, 4), ("q", 1, 0, 4), ("v", 1, 0, 4))
 
 ORDER = (
-    ("T", "q", 0, 0, 1), ("EA", "q", 0, 0, 1), ("T", "k", 0, 0, 2), ("T", "k", 0, 2, 1),
-    ("Q", "q", 0, 0, 1), ("ED", "k", 0, 0, 2), ("T", "k", 0, 3, 1), ("EA", "k", 0, 2, 1),
-    ("T", "q", 0, 1, 1), ("EA", "k", 0, 3, 1), ("T", "q", 0, 2, 2), ("EA", "q", 0, 1, 1),
-    ("Q", "k", 0, 0, 2), ("T", "k", 1, 0, 2), ("Q", "k", 0, 2, 1), ("Q", "k", 0, 3, 1),
-    ("EA", "q", 0, 2, 2), ("Q", "q", 0, 1, 1), ("S", "", 0, 0, 0), ("EA", "k", 1, 0, 2),
-    ("Q", "q", 0, 2, 2), ("S", "", 1, 0, 0), ("XS", "", 0, 0, 0), ("ST", "", 0, 0, 0),
-    ("Q", "k", 1, 0, 2), ("VD", "v", 0, 0, 4), ("XS", "", 1, 0, 0), ("T", "k", 1, 2, 2),
-    ("SW", "", 0, 0, 1), ("S", "", 2, 0, 0), ("XST", "", 0, 0, 0), ("ST", "", 1, 0, 0),
-    ("SW", "", 1, 0, 1), ("ED", "k", 1, 2, 2), ("XS", "", 2, 0, 0), ("T", "q", 1, 0, 2),
-    ("Q", "v", 0, 0, 4), ("S", "", 3, 0, 0), ("XST", "", 1, 0, 0), ("ST", "", 2, 0, 0),
-    ("SW", "", 2, 0, 1), ("QW", "", 0, 0, 1), ("EA", "q", 1, 0, 2), ("ST", "", 3, 0, 0),
-    ("Q", "k", 1, 2, 2), ("O", "", 0, 0, 0), ("QW", "", 1, 0, 1), ("XS", "", 3, 0, 0),
-    ("T", "q", 1, 2, 2), ("Q", "q", 1, 0, 2), ("XST", "", 2, 0, 0), ("EOD", "", 0, 0, 512),
-    ("SW", "", 3, 0, 1), ("S", "", 4, 0, 0), ("XST", "", 3, 0, 0), ("ED", "q", 1, 2, 2),
-    ("O", "", 1, 0, 0), ("ST", "", 4, 0, 0), ("SO", "", 0, 0, 512), ("XS", "", 4, 0, 0),
-    ("EOD", "", 1, 0, 512), ("S", "", 5, 0, 0), ("XST", "", 4, 0, 0), ("QW", "", 2, 0, 1),
-    ("Q", "q", 1, 2, 2), ("SW", "", 4, 0, 1), ("SO", "", 1, 0, 512), ("O", "", 2, 0, 0),
-    ("QW", "", 3, 0, 1), ("XS", "", 5, 0, 0), ("VD", "v", 1, 0, 4), ("ST", "", 5, 0, 0),
-    ("O", "", 3, 0, 0), ("XST", "", 5, 0, 0), ("S", "", 6, 0, 0), ("SW", "", 5, 0, 1),
-    ("ST", "", 6, 0, 0), ("EOD", "", 2, 0, 512), ("XS", "", 6, 0, 0), ("S", "", 7, 0, 0),
-    ("ST", "", 7, 0, 0), ("QW", "", 4, 0, 1), ("XST", "", 6, 0, 0), ("Q", "v", 1, 0, 4),
-    ("SW", "", 6, 0, 1), ("SO", "", 2, 0, 512), ("XST", "", 7, 0, 0), ("EOD", "", 3, 0, 512),
-    ("O", "", 4, 0, 0), ("XS", "", 7, 0, 0), ("QW", "", 5, 0, 1), ("QW", "", 6, 0, 1),
-    ("SO", "", 3, 0, 512), ("QW", "", 7, 0, 1), ("EOA", "", 4, 0, 512), ("O", "", 5, 0, 0),
-    ("O", "", 6, 0, 0), ("SW", "", 7, 0, 1), ("EOD", "", 5, 0, 512), ("O", "", 7, 0, 0),
-    ("EOA", "", 6, 0, 512), ("SO", "", 4, 0, 512), ("EOD", "", 7, 0, 256), ("EOA", "", 7, 256, 256),
-    ("SO", "", 5, 0, 512), ("SO", "", 6, 0, 512), ("SO", "", 7, 0, 512),
+    ("D", "", 128, 0, 0), ("D", "", 128, 0, 0), ("D", "", 128, 0, 0), ("D", "", 128, 0, 0),
+    ("T", "q", 0, 0, 1), ("D", "", 64, 0, 0), ("ED", "q", 0, 0, 1), ("T", "k", 0, 0, 2),
+    ("D", "", 64, 0, 0), ("T", "k", 0, 2, 1), ("Q", "q", 0, 0, 1), ("D", "", 64, 0, 0),
+    ("EA", "k", 0, 0, 2), ("T", "k", 0, 3, 1), ("D", "", 64, 0, 0), ("ED", "k", 0, 2, 1),
+    ("T", "q", 0, 1, 1), ("D", "", 64, 0, 0), ("EA", "k", 0, 3, 1), ("EA", "q", 0, 1, 1),
+    ("Q", "k", 0, 0, 2), ("T", "q", 0, 2, 2), ("Q", "k", 0, 2, 2), ("D", "", 64, 0, 0),
+    ("T", "k", 1, 0, 2), ("ED", "q", 0, 2, 2), ("S", "", 0, 0, 0), ("Q", "q", 0, 1, 1),
+    ("EA", "k", 1, 0, 2), ("ST", "", 0, 0, 0), ("Q", "q", 0, 2, 2), ("S", "", 1, 0, 0),
+    ("XS", "", 0, 0, 0), ("ST", "", 1, 0, 0), ("Q", "k", 1, 0, 2), ("ST", "", 2, 0, 0),
+    ("XST", "", 0, 0, 0), ("VD", "v", 0, 0, 4), ("T", "k", 1, 2, 2), ("SW", "", 0, 0, 1),
+    ("XS", "", 1, 0, 0), ("T", "q", 1, 0, 2), ("XST", "", 1, 0, 0), ("S", "", 2, 0, 0),
+    ("QW", "", 0, 0, 1), ("SW", "", 1, 0, 1), ("ED", "k", 1, 2, 2), ("XST", "", 2, 0, 0),
+    ("S", "", 3, 0, 0), ("T", "q", 1, 2, 2), ("Q", "v", 0, 0, 4), ("EA", "q", 1, 0, 2),
+    ("Q", "k", 1, 2, 2), ("XS", "", 2, 0, 0), ("O", "", 0, 0, 0), ("QW", "", 1, 0, 1),
+    ("Q", "q", 1, 0, 2), ("XS", "", 3, 0, 0), ("O", "", 1, 0, 0), ("QW", "", 2, 0, 1),
+    ("SW", "", 2, 0, 1), ("EOD", "", 0, 0, 512), ("EA", "q", 1, 2, 2), ("S", "", 4, 0, 0),
+    ("S", "", 5, 0, 0), ("SW", "", 3, 0, 1), ("EOD", "", 1, 0, 512), ("ST", "", 4, 0, 0),
+    ("XS", "", 4, 0, 0), ("SO", "", 0, 0, 512), ("O", "", 2, 0, 0), ("Q", "q", 1, 2, 2),
+    ("ST", "", 3, 0, 0), ("XS", "", 5, 0, 0), ("VD", "v", 1, 0, 4), ("SO", "", 1, 0, 512),
+    ("SW", "", 4, 0, 1), ("S", "", 6, 0, 0), ("XST", "", 4, 0, 0), ("ST", "", 5, 0, 0),
+    ("SW", "", 5, 0, 1), ("S", "", 7, 0, 0), ("XST", "", 3, 0, 0), ("ST", "", 6, 0, 0),
+    ("EOD", "", 2, 0, 512), ("ST", "", 7, 0, 0), ("XS", "", 6, 0, 0), ("QW", "", 3, 0, 1),
+    ("XST", "", 5, 0, 0), ("QW", "", 4, 0, 1), ("Q", "v", 1, 0, 4), ("O", "", 3, 0, 0),
+    ("SW", "", 6, 0, 1), ("SO", "", 2, 0, 512), ("XS", "", 7, 0, 0), ("QW", "", 5, 0, 1),
+    ("EOD", "", 3, 0, 512), ("O", "", 4, 0, 0), ("XST", "", 6, 0, 0), ("O", "", 5, 0, 0),
+    ("SW", "", 7, 0, 1), ("XST", "", 7, 0, 0), ("EOD", "", 4, 0, 512), ("SO", "", 3, 0, 512),
+    ("EOA", "", 5, 0, 512), ("QW", "", 6, 0, 1), ("QW", "", 7, 0, 1), ("SO", "", 4, 0, 512),
+    ("O", "", 6, 0, 0), ("O", "", 7, 0, 0), ("SO", "", 5, 0, 512), ("EOA", "", 6, 0, 256),
+    ("EOD", "", 6, 256, 256), ("EOD", "", 7, 0, 512), ("SO", "", 6, 0, 512), ("SO", "", 7, 0, 512),
 )
 
 
@@ -154,16 +156,13 @@ def tile_curveattention_kernel(tc, query, key, value, out_0, out_1):
         def keep_clock(n):
             nc.tensor.matmul(idle_bank[:, :n], lhsT=zeros[:], rhs=zeros[:, :n], start=True, stop=True)
 
-        for i in range(4):
-            keep_clock(P)
-
         def step(kind, nm, i, a, b):
             h, tq = i // NT, i % NT
             q0 = tq * P
-            if kind == "T":
+            if kind == "D":
+                keep_clock(i)
+            elif kind == "T":
                 flip(nm, i, a, b)
-                if i == 0:
-                    keep_clock(64)
             elif kind == "EA" or kind == "ED":
                 flip_out(nm, i, a, b, kind[1])
             elif kind == "VP" or kind == "VD":

@@ -28,34 +28,34 @@ LOADS = (("q", 0, 0, 1), ("k", 0, 0, 2), ("k", 0, 2, 1), ("k", 0, 3, 1), ("q", 0
 
 ORDER = (
     ("D", "", 128, 0, 0), ("D", "", 128, 0, 0), ("D", "", 128, 0, 0), ("D", "", 128, 0, 0),
-    ("T", "q", 0, 0, 1), ("D", "", 64, 0, 0), ("ED", "q", 0, 0, 1), ("T", "k", 0, 0, 2),
-    ("D", "", 64, 0, 0), ("T", "k", 0, 2, 1), ("Q", "q", 0, 0, 1), ("D", "", 64, 0, 0),
-    ("EA", "k", 0, 0, 2), ("T", "k", 0, 3, 1), ("D", "", 64, 0, 0), ("ED", "k", 0, 2, 1),
-    ("T", "q", 0, 1, 1), ("D", "", 64, 0, 0), ("EA", "k", 0, 3, 1), ("EA", "q", 0, 1, 1),
-    ("Q", "k", 0, 0, 2), ("T", "q", 0, 2, 2), ("Q", "k", 0, 2, 2), ("D", "", 64, 0, 0),
-    ("T", "k", 1, 0, 2), ("ED", "q", 0, 2, 2), ("S", "", 0, 0, 0), ("Q", "q", 0, 1, 1),
-    ("EA", "k", 1, 0, 2), ("ST", "", 0, 0, 0), ("Q", "q", 0, 2, 2), ("S", "", 1, 0, 0),
-    ("XS", "", 0, 0, 0), ("ST", "", 1, 0, 0), ("Q", "k", 1, 0, 2), ("ST", "", 2, 0, 0),
-    ("XST", "", 0, 0, 0), ("VD", "v", 0, 0, 4), ("T", "k", 1, 2, 2), ("SW", "", 0, 0, 1),
-    ("XS", "", 1, 0, 0), ("T", "q", 1, 0, 2), ("XST", "", 1, 0, 0), ("S", "", 2, 0, 0),
-    ("QW", "", 0, 0, 1), ("SW", "", 1, 0, 1), ("ED", "k", 1, 2, 2), ("XST", "", 2, 0, 0),
-    ("S", "", 3, 0, 0), ("T", "q", 1, 2, 2), ("Q", "v", 0, 0, 4), ("EA", "q", 1, 0, 2),
-    ("Q", "k", 1, 2, 2), ("XS", "", 2, 0, 0), ("O", "", 0, 0, 0), ("QW", "", 1, 0, 1),
-    ("Q", "q", 1, 0, 2), ("XS", "", 3, 0, 0), ("O", "", 1, 0, 0), ("QW", "", 2, 0, 1),
-    ("SW", "", 2, 0, 1), ("EOD", "", 0, 0, 512), ("EA", "q", 1, 2, 2), ("S", "", 4, 0, 0),
-    ("S", "", 5, 0, 0), ("SW", "", 3, 0, 1), ("EOD", "", 1, 0, 512), ("ST", "", 4, 0, 0),
-    ("XS", "", 4, 0, 0), ("SO", "", 0, 0, 512), ("O", "", 2, 0, 0), ("Q", "q", 1, 2, 2),
-    ("ST", "", 3, 0, 0), ("XS", "", 5, 0, 0), ("VD", "v", 1, 0, 4), ("SO", "", 1, 0, 512),
-    ("SW", "", 4, 0, 1), ("S", "", 6, 0, 0), ("XST", "", 4, 0, 0), ("ST", "", 5, 0, 0),
-    ("SW", "", 5, 0, 1), ("S", "", 7, 0, 0), ("XST", "", 3, 0, 0), ("ST", "", 6, 0, 0),
-    ("EOD", "", 2, 0, 512), ("ST", "", 7, 0, 0), ("XS", "", 6, 0, 0), ("QW", "", 3, 0, 1),
-    ("XST", "", 5, 0, 0), ("QW", "", 4, 0, 1), ("Q", "v", 1, 0, 4), ("O", "", 3, 0, 0),
-    ("SW", "", 6, 0, 1), ("SO", "", 2, 0, 512), ("XS", "", 7, 0, 0), ("QW", "", 5, 0, 1),
-    ("EOD", "", 3, 0, 512), ("O", "", 4, 0, 0), ("XST", "", 6, 0, 0), ("O", "", 5, 0, 0),
-    ("SW", "", 7, 0, 1), ("XST", "", 7, 0, 0), ("EOD", "", 4, 0, 512), ("SO", "", 3, 0, 512),
-    ("EOA", "", 5, 0, 512), ("QW", "", 6, 0, 1), ("QW", "", 7, 0, 1), ("SO", "", 4, 0, 512),
-    ("O", "", 6, 0, 0), ("O", "", 7, 0, 0), ("SO", "", 5, 0, 512), ("EOA", "", 6, 0, 256),
-    ("EOD", "", 6, 256, 256), ("EOD", "", 7, 0, 512), ("SO", "", 6, 0, 512), ("SO", "", 7, 0, 512),
+    ("D", "", 128, 0, 0), ("T", "q", 0, 0, 1), ("D", "", 64, 0, 0), ("ED", "q", 0, 0, 1),
+    ("T", "k", 0, 0, 2), ("D", "", 64, 0, 0), ("Q", "q", 0, 0, 1), ("T", "k", 0, 2, 1),
+    ("EA", "k", 0, 0, 2), ("D", "", 64, 0, 0), ("T", "k", 0, 3, 1), ("ED", "k", 0, 2, 1),
+    ("D", "", 64, 0, 0), ("T", "q", 0, 1, 1), ("EA", "k", 0, 3, 1), ("D", "", 64, 0, 0),
+    ("Q", "k", 0, 0, 2), ("EA", "q", 0, 1, 1), ("T", "q", 0, 2, 2), ("Q", "k", 0, 2, 2),
+    ("D", "", 64, 0, 0), ("ED", "q", 0, 2, 2), ("T", "k", 1, 0, 2), ("S", "", 0, 0, 0),
+    ("Q", "q", 0, 1, 1), ("EA", "k", 1, 0, 2), ("ST", "", 0, 0, 0), ("Q", "q", 0, 2, 2),
+    ("S", "", 1, 0, 0), ("XS", "", 0, 0, 0), ("ST", "", 1, 0, 0), ("Q", "k", 1, 0, 2),
+    ("ST", "", 2, 0, 0), ("XST", "", 0, 0, 0), ("VD", "v", 0, 0, 4), ("T", "k", 1, 2, 2),
+    ("SW", "", 0, 0, 1), ("XS", "", 1, 0, 0), ("XST", "", 1, 0, 0), ("T", "q", 1, 0, 2),
+    ("QW", "", 0, 0, 1), ("SW", "", 1, 0, 1), ("S", "", 2, 0, 0), ("ED", "k", 1, 2, 2),
+    ("XST", "", 2, 0, 0), ("S", "", 3, 0, 0), ("Q", "v", 0, 0, 4), ("T", "q", 1, 2, 2),
+    ("EA", "q", 1, 0, 2), ("Q", "k", 1, 2, 2), ("XS", "", 2, 0, 0), ("QW", "", 1, 0, 1),
+    ("O", "", 0, 0, 0), ("Q", "q", 1, 0, 2), ("XS", "", 3, 0, 0), ("QW", "", 2, 0, 1),
+    ("O", "", 1, 0, 0), ("SW", "", 2, 0, 1), ("EOD", "", 0, 0, 512), ("EA", "q", 1, 2, 2),
+    ("S", "", 4, 0, 0), ("S", "", 5, 0, 0), ("SW", "", 3, 0, 1), ("EOD", "", 1, 0, 512),
+    ("ST", "", 4, 0, 0), ("XS", "", 4, 0, 0), ("SO", "", 0, 0, 512), ("O", "", 2, 0, 0),
+    ("Q", "q", 1, 2, 2), ("XS", "", 5, 0, 0), ("ST", "", 3, 0, 0), ("VD", "v", 1, 0, 4),
+    ("SO", "", 1, 0, 512), ("SW", "", 4, 0, 1), ("S", "", 6, 0, 0), ("XST", "", 4, 0, 0),
+    ("ST", "", 5, 0, 0), ("SW", "", 5, 0, 1), ("S", "", 7, 0, 0), ("XST", "", 3, 0, 0),
+    ("ST", "", 6, 0, 0), ("EOD", "", 2, 0, 512), ("XS", "", 6, 0, 0), ("ST", "", 7, 0, 0),
+    ("QW", "", 3, 0, 1), ("XST", "", 5, 0, 0), ("QW", "", 4, 0, 1), ("Q", "v", 1, 0, 4),
+    ("SW", "", 6, 0, 1), ("O", "", 3, 0, 0), ("SO", "", 2, 0, 512), ("XS", "", 7, 0, 0),
+    ("QW", "", 5, 0, 1), ("EOD", "", 3, 0, 512), ("XST", "", 6, 0, 0), ("O", "", 4, 0, 0),
+    ("O", "", 5, 0, 0), ("SW", "", 7, 0, 1), ("XST", "", 7, 0, 0), ("EOD", "", 4, 0, 512),
+    ("SO", "", 3, 0, 512), ("EOA", "", 5, 0, 512), ("QW", "", 6, 0, 1), ("QW", "", 7, 0, 1),
+    ("SO", "", 4, 0, 512), ("O", "", 6, 0, 0), ("O", "", 7, 0, 0), ("SO", "", 5, 0, 512),
+    ("EOD", "", 6, 0, 512), ("EOA", "", 7, 0, 512), ("SO", "", 6, 0, 512), ("SO", "", 7, 0, 512),
 )
 
 

@@ -24,37 +24,37 @@ FLOPS = 2 * 2 * HEADS * S * S * D
 SCALE = D ** (-0.5)
 NEG_LOG_C = -math.log(1.0 + math.exp(math.exp(1.0)))
 
-LOADS = (("q", 0, 0, 1), ("k", 0, 0, 2), ("k", 0, 2, 1), ("k", 0, 3, 1), ("q", 0, 1, 1), ("q", 0, 2, 2), ("k", 1, 0, 2), ("k", 1, 2, 2), ("v", 0, 0, 4), ("q", 1, 0, 4), ("v", 1, 0, 4))
+LOADS = (("q", 0, 0, 1), ("k", 0, 0, 2), ("k", 0, 2, 2), ("q", 0, 1, 3), ("k", 1, 0, 2), ("k", 1, 2, 2), ("v", 0, 0, 4), ("q", 1, 0, 4), ("v", 1, 0, 4))
 
 ORDER = (
     ("D", "", 128, 0, 0), ("D", "", 128, 0, 0), ("D", "", 128, 0, 0), ("D", "", 128, 0, 0),
     ("D", "", 128, 0, 0), ("T", "q", 0, 0, 1), ("D", "", 64, 0, 0), ("ED", "q", 0, 0, 1),
-    ("T", "k", 0, 0, 2), ("D", "", 64, 0, 0), ("Q", "q", 0, 0, 1), ("T", "k", 0, 2, 1),
-    ("EA", "k", 0, 0, 2), ("D", "", 64, 0, 0), ("T", "k", 0, 3, 1), ("ED", "k", 0, 2, 1),
-    ("D", "", 64, 0, 0), ("T", "q", 0, 1, 1), ("EA", "k", 0, 3, 1), ("D", "", 64, 0, 0),
-    ("Q", "k", 0, 0, 2), ("EA", "q", 0, 1, 1), ("T", "q", 0, 2, 2), ("Q", "k", 0, 2, 2),
-    ("D", "", 64, 0, 0), ("ED", "q", 0, 2, 2), ("T", "k", 1, 0, 2), ("S", "", 0, 0, 0),
-    ("Q", "q", 0, 1, 1), ("EA", "k", 1, 0, 2), ("ST", "", 0, 0, 0), ("Q", "q", 0, 2, 2),
-    ("S", "", 1, 0, 0), ("XS", "", 0, 0, 0), ("ST", "", 1, 0, 0), ("Q", "k", 1, 0, 2),
-    ("ST", "", 2, 0, 0), ("XST", "", 0, 0, 0), ("VD", "v", 0, 0, 4), ("T", "k", 1, 2, 2),
-    ("SW", "", 0, 0, 1), ("XS", "", 1, 0, 0), ("XST", "", 1, 0, 0), ("T", "q", 1, 0, 2),
-    ("QW", "", 0, 0, 1), ("SW", "", 1, 0, 1), ("S", "", 2, 0, 0), ("ED", "k", 1, 2, 2),
-    ("XST", "", 2, 0, 0), ("S", "", 3, 0, 0), ("Q", "v", 0, 0, 4), ("T", "q", 1, 2, 2),
-    ("EA", "q", 1, 0, 2), ("Q", "k", 1, 2, 2), ("XS", "", 2, 0, 0), ("QW", "", 1, 0, 1),
-    ("O", "", 0, 0, 0), ("Q", "q", 1, 0, 2), ("XS", "", 3, 0, 0), ("QW", "", 2, 0, 1),
-    ("O", "", 1, 0, 0), ("SW", "", 2, 0, 1), ("EOD", "", 0, 0, 512), ("EA", "q", 1, 2, 2),
-    ("S", "", 4, 0, 0), ("S", "", 5, 0, 0), ("SW", "", 3, 0, 1), ("EOD", "", 1, 0, 512),
-    ("ST", "", 4, 0, 0), ("XS", "", 4, 0, 0), ("SO", "", 0, 0, 512), ("O", "", 2, 0, 0),
-    ("Q", "q", 1, 2, 2), ("XS", "", 5, 0, 0), ("ST", "", 3, 0, 0), ("VD", "v", 1, 0, 4),
-    ("SO", "", 1, 0, 512), ("SW", "", 4, 0, 1), ("S", "", 6, 0, 0), ("XST", "", 4, 0, 0),
-    ("ST", "", 5, 0, 0), ("SW", "", 5, 0, 1), ("S", "", 7, 0, 0), ("XST", "", 3, 0, 0),
-    ("ST", "", 6, 0, 0), ("EOD", "", 2, 0, 512), ("XS", "", 6, 0, 0), ("ST", "", 7, 0, 0),
-    ("QW", "", 3, 0, 1), ("XST", "", 5, 0, 0), ("QW", "", 4, 0, 1), ("Q", "v", 1, 0, 4),
-    ("SW", "", 6, 0, 1), ("O", "", 3, 0, 0), ("SO", "", 2, 0, 512), ("XS", "", 7, 0, 0),
-    ("QW", "", 5, 0, 1), ("EOD", "", 3, 0, 512), ("XST", "", 6, 0, 0), ("O", "", 4, 0, 0),
-    ("O", "", 5, 0, 0), ("SW", "", 7, 0, 1), ("XST", "", 7, 0, 0), ("EOD", "", 4, 0, 512),
+    ("T", "k", 0, 0, 2), ("D", "", 64, 0, 0), ("Q", "q", 0, 0, 1), ("EA", "k", 0, 0, 2),
+    ("T", "k", 0, 2, 1), ("D", "", 64, 0, 0), ("T", "k", 0, 3, 1), ("ED", "k", 0, 2, 1),
+    ("D", "", 64, 0, 0), ("EA", "k", 0, 3, 1), ("Q", "k", 0, 0, 2), ("T", "q", 0, 1, 1),
+    ("D", "", 64, 0, 0), ("T", "q", 0, 2, 2), ("EA", "q", 0, 1, 1), ("Q", "k", 0, 2, 2),
+    ("D", "", 64, 0, 0), ("T", "k", 1, 0, 2), ("ED", "q", 0, 2, 2), ("S", "", 0, 0, 0),
+    ("EA", "k", 1, 0, 2), ("Q", "q", 0, 1, 1), ("ST", "", 0, 0, 0), ("Q", "q", 0, 2, 2),
+    ("XS", "", 0, 0, 0), ("S", "", 1, 0, 0), ("Q", "k", 1, 0, 2), ("ST", "", 1, 0, 0),
+    ("XST", "", 0, 0, 0), ("VD", "v", 0, 0, 4), ("S", "", 2, 0, 0), ("SW", "", 0, 0, 1),
+    ("T", "k", 1, 2, 2), ("XS", "", 1, 0, 0), ("T", "q", 1, 0, 2), ("XST", "", 1, 0, 0),
+    ("S", "", 3, 0, 0), ("QW", "", 0, 0, 1), ("SW", "", 1, 0, 1), ("ED", "k", 1, 2, 2),
+    ("XS", "", 2, 0, 0), ("ST", "", 2, 0, 0), ("T", "q", 1, 2, 2), ("Q", "v", 0, 0, 4),
+    ("EA", "q", 1, 0, 2), ("SW", "", 2, 0, 1), ("Q", "k", 1, 2, 2), ("XS", "", 3, 0, 0),
+    ("QW", "", 1, 0, 1), ("O", "", 0, 0, 0), ("Q", "q", 1, 0, 2), ("XST", "", 2, 0, 0),
+    ("O", "", 1, 0, 0), ("SW", "", 3, 0, 1), ("EOD", "", 0, 0, 512), ("EA", "q", 1, 2, 2),
+    ("S", "", 4, 0, 0), ("S", "", 5, 0, 0), ("EOD", "", 1, 0, 512), ("ST", "", 4, 0, 0),
+    ("XS", "", 4, 0, 0), ("SO", "", 0, 0, 512), ("ST", "", 3, 0, 0), ("QW", "", 2, 0, 1),
+    ("XS", "", 5, 0, 0), ("Q", "q", 1, 2, 2), ("SO", "", 1, 0, 512), ("SW", "", 4, 0, 1),
+    ("VD", "v", 1, 0, 4), ("O", "", 2, 0, 0), ("XST", "", 4, 0, 0), ("S", "", 6, 0, 0),
+    ("SW", "", 5, 0, 1), ("ST", "", 5, 0, 0), ("XST", "", 3, 0, 0), ("S", "", 7, 0, 0),
+    ("ST", "", 6, 0, 0), ("XS", "", 6, 0, 0), ("EOD", "", 2, 0, 512), ("ST", "", 7, 0, 0),
+    ("XST", "", 5, 0, 0), ("QW", "", 3, 0, 1), ("QW", "", 4, 0, 1), ("SW", "", 6, 0, 1),
+    ("Q", "v", 1, 0, 4), ("SO", "", 2, 0, 512), ("XS", "", 7, 0, 0), ("O", "", 3, 0, 0),
+    ("QW", "", 5, 0, 1), ("XST", "", 6, 0, 0), ("EOD", "", 3, 0, 512), ("O", "", 4, 0, 0),
+    ("SW", "", 7, 0, 1), ("O", "", 5, 0, 0), ("XST", "", 7, 0, 0), ("EOD", "", 4, 0, 512),
     ("SO", "", 3, 0, 512), ("EOA", "", 5, 0, 512), ("QW", "", 6, 0, 1), ("QW", "", 7, 0, 1),
-    ("SO", "", 4, 0, 512), ("O", "", 6, 0, 0), ("O", "", 7, 0, 0), ("SO", "", 5, 0, 512),
+    ("SO", "", 4, 0, 512), ("O", "", 6, 0, 0), ("SO", "", 5, 0, 512), ("O", "", 7, 0, 0),
     ("EOD", "", 6, 0, 512), ("EOA", "", 7, 0, 512), ("SO", "", 6, 0, 512), ("SO", "", 7, 0, 512),
 )
 

@@ -27,13 +27,13 @@ NEG_LOG_C = -math.log(1.0 + math.exp(math.exp(1.0)))
 LOADS = (("q", 0, 0, 1), ("k", 0, 0, 2), ("k", 0, 2, 2), ("q", 0, 1, 3), ("k", 1, 0, 2), ("k", 1, 2, 2), ("v", 0, 0, 4), ("q", 1, 0, 4), ("v", 1, 0, 4))
 
 ORDER = (
-    ("D", "", 128, 0, 0), ("D", "", 128, 0, 0), ("D", "", 128, 0, 0), ("D", "", 128, 0, 0),
-    ("D", "", 128, 0, 0), ("T", "q", 0, 0, 1), ("D", "", 64, 0, 0), ("ED", "q", 0, 0, 1),
-    ("T", "k", 0, 0, 2), ("D", "", 64, 0, 0), ("Q", "q", 0, 0, 1), ("EA", "k", 0, 0, 2),
-    ("T", "k", 0, 2, 1), ("D", "", 64, 0, 0), ("T", "k", 0, 3, 1), ("ED", "k", 0, 2, 1),
-    ("D", "", 64, 0, 0), ("EA", "k", 0, 3, 1), ("Q", "k", 0, 0, 2), ("T", "q", 0, 1, 1),
-    ("D", "", 64, 0, 0), ("T", "q", 0, 2, 2), ("EA", "q", 0, 1, 1), ("Q", "k", 0, 2, 2),
-    ("D", "", 64, 0, 0), ("T", "k", 1, 0, 2), ("ED", "q", 0, 2, 2), ("S", "", 0, 0, 0),
+
+    ("T", "q", 0, 0, 1), ("D", "", 96, 0, 0), ("ED", "q", 0, 0, 1),
+    ("T", "k", 0, 0, 2), ("D", "", 96, 0, 0), ("Q", "q", 0, 0, 1), ("EA", "k", 0, 0, 2),
+    ("T", "k", 0, 2, 1), ("D", "", 96, 0, 0), ("T", "k", 0, 3, 1), ("ED", "k", 0, 2, 1),
+    ("D", "", 96, 0, 0), ("EA", "k", 0, 3, 1), ("Q", "k", 0, 0, 2), ("T", "q", 0, 1, 1),
+    ("D", "", 96, 0, 0), ("T", "q", 0, 2, 2), ("EA", "q", 0, 1, 1), ("Q", "k", 0, 2, 2),
+    ("D", "", 96, 0, 0), ("T", "k", 1, 0, 2), ("ED", "q", 0, 2, 2), ("S", "", 0, 0, 0),
     ("EA", "k", 1, 0, 2), ("Q", "q", 0, 1, 1), ("ST", "", 0, 0, 0), ("Q", "q", 0, 2, 2),
     ("XS", "", 0, 0, 0), ("S", "", 1, 0, 0), ("Q", "k", 1, 0, 2), ("ST", "", 1, 0, 0),
     ("XST", "", 0, 0, 0), ("VD", "v", 0, 0, 4), ("S", "", 2, 0, 0), ("SW", "", 0, 0, 1),
@@ -69,6 +69,8 @@ def tile_curveattention_kernel(tc, query, key, value, out_0, out_1):
 
         ident = keep.tile([P, P], F32, name="ident")
         make_identity(nc, ident[:])
+        zeros16 = keep.tile([P, 512], BF16, name="zeros16")
+        nc.vector.memset(zeros16[:], 0.0)
         warm = keep.tile([P, 1], F32, name="warm")
         nc.vector.memset(warm[:], 0.0)
         zeros = keep.tile([P, P], F32, name="zeros")
@@ -155,6 +157,9 @@ def tile_curveattention_kernel(tc, query, key, value, out_0, out_1):
 
         def keep_clock(n):
             nc.tensor.matmul(idle_bank[:, :n], lhsT=zeros[:], rhs=zeros[:, :n], start=True, stop=True)
+
+        for i in range(4):
+            nc.tensor.matmul(idle_bank[:], lhsT=zeros16[:, :P], rhs=zeros16[:], start=True, stop=True)
 
         def step(kind, nm, i, a, b):
             h, tq = i // NT, i % NT

@@ -10,8 +10,6 @@ U32 = mybir.dt.uint32
 U8 = mybir.dt.uint8
 FP8X4 = mybir.dt.float8_e4m3fn_x4
 EXP = mybir.ActivationFunctionType.Exp
-MULT = mybir.AluOpType.mult
-ADD = mybir.AluOpType.add
 
 P = 128
 PACK = 4
@@ -27,31 +25,30 @@ NEG_LOG_C = -math.log(1.0 + math.exp(math.exp(1.0)))
 LOADS = (("q", 0, 0, 1), ("k", 0, 0, 2), ("k", 0, 2, 2), ("q", 0, 1, 3), ("k", 1, 0, 2), ("k", 1, 2, 2), ("v", 0, 0, 4), ("q", 1, 0, 4), ("v", 1, 0, 4))
 
 ORDER = (
-
-    ("T", "q", 0, 0, 1), ("D", "", 96, 0, 0), ("ED", "q", 0, 0, 1),
-    ("T", "k", 0, 0, 2), ("D", "", 96, 0, 0), ("Q", "q", 0, 0, 1), ("EA", "k", 0, 0, 2),
-    ("T", "k", 0, 2, 1), ("D", "", 96, 0, 0), ("T", "k", 0, 3, 1), ("ED", "k", 0, 2, 1),
-    ("D", "", 96, 0, 0), ("EA", "k", 0, 3, 1), ("Q", "k", 0, 0, 2), ("T", "q", 0, 1, 1),
-    ("D", "", 96, 0, 0), ("T", "q", 0, 2, 2), ("EA", "q", 0, 1, 1), ("Q", "k", 0, 2, 2),
-    ("D", "", 96, 0, 0), ("T", "k", 1, 0, 2), ("ED", "q", 0, 2, 2), ("S", "", 0, 0, 0),
-    ("EA", "k", 1, 0, 2), ("Q", "q", 0, 1, 1), ("ST", "", 0, 0, 0), ("Q", "q", 0, 2, 2),
-    ("XS", "", 0, 0, 0), ("S", "", 1, 0, 0), ("Q", "k", 1, 0, 2), ("ST", "", 1, 0, 0),
-    ("XST", "", 0, 0, 0), ("VD", "v", 0, 0, 4), ("S", "", 2, 0, 0), ("SW", "", 0, 0, 1),
-    ("T", "k", 1, 2, 2), ("XS", "", 1, 0, 0), ("T", "q", 1, 0, 2), ("XST", "", 1, 0, 0),
-    ("S", "", 3, 0, 0), ("QW", "", 0, 0, 1), ("SW", "", 1, 0, 1), ("ED", "k", 1, 2, 2),
-    ("XS", "", 2, 0, 0), ("ST", "", 2, 0, 0), ("T", "q", 1, 2, 2), ("Q", "v", 0, 0, 4),
-    ("EA", "q", 1, 0, 2), ("SW", "", 2, 0, 1), ("Q", "k", 1, 2, 2), ("XS", "", 3, 0, 0),
-    ("QW", "", 1, 0, 1), ("O", "", 0, 0, 0), ("Q", "q", 1, 0, 2), ("XST", "", 2, 0, 0),
-    ("O", "", 1, 0, 0), ("SW", "", 3, 0, 1), ("EOD", "", 0, 0, 512), ("EA", "q", 1, 2, 2),
-    ("S", "", 4, 0, 0), ("S", "", 5, 0, 0), ("EOD", "", 1, 0, 512), ("ST", "", 4, 0, 0),
-    ("XS", "", 4, 0, 0), ("SO", "", 0, 0, 512), ("ST", "", 3, 0, 0), ("QW", "", 2, 0, 1),
-    ("XS", "", 5, 0, 0), ("Q", "q", 1, 2, 2), ("SO", "", 1, 0, 512), ("SW", "", 4, 0, 1),
-    ("VD", "v", 1, 0, 4), ("O", "", 2, 0, 0), ("XST", "", 4, 0, 0), ("S", "", 6, 0, 0),
-    ("SW", "", 5, 0, 1), ("ST", "", 5, 0, 0), ("XST", "", 3, 0, 0), ("S", "", 7, 0, 0),
-    ("ST", "", 6, 0, 0), ("XS", "", 6, 0, 0), ("EOD", "", 2, 0, 512), ("ST", "", 7, 0, 0),
-    ("XST", "", 5, 0, 0), ("QW", "", 3, 0, 1), ("QW", "", 4, 0, 1), ("SW", "", 6, 0, 1),
-    ("Q", "v", 1, 0, 4), ("SO", "", 2, 0, 512), ("XS", "", 7, 0, 0), ("O", "", 3, 0, 0),
-    ("QW", "", 5, 0, 1), ("XST", "", 6, 0, 0), ("EOD", "", 3, 0, 512), ("O", "", 4, 0, 0),
+    ("T", "q", 0, 0, 1), ("D", "", 96, 0, 0), ("EA", "q", 0, 0, 1), ("T", "k", 0, 0, 2),
+    ("D", "", 96, 0, 0), ("ED", "k", 0, 0, 2), ("T", "k", 0, 2, 1), ("D", "", 96, 0, 0),
+    ("T", "k", 0, 3, 1), ("EA", "k", 0, 2, 1), ("D", "", 96, 0, 0), ("Q", "q", 0, 0, 1),
+    ("ED", "k", 0, 3, 1), ("T", "q", 0, 1, 1), ("D", "", 96, 0, 0), ("Q", "k", 0, 0, 2),
+    ("T", "q", 0, 2, 2), ("EA", "q", 0, 1, 1), ("Q", "k", 0, 2, 2), ("D", "", 96, 0, 0),
+    ("T", "k", 1, 0, 2), ("ED", "q", 0, 2, 2), ("S", "", 0, 0, 0), ("Q", "q", 0, 1, 1),
+    ("ED", "k", 1, 0, 2), ("XS", "", 0, 0, 0), ("S", "", 1, 0, 0), ("Q", "q", 0, 2, 2),
+    ("ST", "", 0, 0, 0), ("Q", "k", 1, 0, 2), ("XS", "", 1, 0, 0), ("ST", "", 1, 0, 0),
+    ("SW", "", 0, 0, 1), ("VD", "v", 0, 0, 4), ("S", "", 2, 0, 0), ("XST", "", 0, 0, 0),
+    ("T", "k", 1, 2, 2), ("SW", "", 1, 0, 1), ("T", "q", 1, 0, 2), ("XST", "", 1, 0, 0),
+    ("S", "", 3, 0, 0), ("QW", "", 0, 0, 1), ("XS", "", 2, 0, 0), ("T", "q", 1, 2, 2),
+    ("ED", "k", 1, 2, 2), ("EA", "q", 1, 0, 2), ("ST", "", 2, 0, 0), ("Q", "v", 0, 0, 4),
+    ("SW", "", 2, 0, 1), ("XS", "", 3, 0, 0), ("Q", "k", 1, 2, 2), ("QW", "", 1, 0, 1),
+    ("O", "", 0, 0, 0), ("EA", "q", 1, 2, 2), ("Q", "q", 1, 0, 2), ("SW", "", 3, 0, 1),
+    ("O", "", 1, 0, 0), ("EOD", "", 0, 0, 512), ("XST", "", 2, 0, 0), ("S", "", 4, 0, 0),
+    ("S", "", 5, 0, 0), ("EOD", "", 1, 0, 512), ("ST", "", 3, 0, 0), ("XS", "", 4, 0, 0),
+    ("SO", "", 0, 0, 512), ("QW", "", 2, 0, 1), ("Q", "q", 1, 2, 2), ("XS", "", 5, 0, 0),
+    ("SO", "", 1, 0, 512), ("VD", "v", 1, 0, 2), ("O", "", 2, 0, 0), ("SW", "", 4, 0, 1),
+    ("ST", "", 4, 0, 0), ("XST", "", 3, 0, 0), ("S", "", 6, 0, 0), ("SW", "", 5, 0, 1),
+    ("EOD", "", 2, 0, 512), ("ST", "", 5, 0, 0), ("XST", "", 4, 0, 0), ("S", "", 7, 0, 0),
+    ("VD", "v", 1, 2, 2), ("XS", "", 6, 0, 0), ("ST", "", 6, 0, 0), ("SO", "", 2, 0, 512),
+    ("ST", "", 7, 0, 0), ("QW", "", 3, 0, 1), ("XST", "", 5, 0, 0), ("QW", "", 4, 0, 1),
+    ("Q", "v", 1, 0, 4), ("SW", "", 6, 0, 1), ("O", "", 3, 0, 0), ("XS", "", 7, 0, 0),
+    ("QW", "", 5, 0, 1), ("EOD", "", 3, 0, 512), ("XST", "", 6, 0, 0), ("O", "", 4, 0, 0),
     ("SW", "", 7, 0, 1), ("O", "", 5, 0, 0), ("XST", "", 7, 0, 0), ("EOD", "", 4, 0, 512),
     ("SO", "", 3, 0, 512), ("EOA", "", 5, 0, 512), ("QW", "", 6, 0, 1), ("QW", "", 7, 0, 1),
     ("SO", "", 4, 0, 512), ("O", "", 6, 0, 0), ("SO", "", 5, 0, 512), ("O", "", 7, 0, 0),
@@ -69,7 +66,7 @@ def tile_curveattention_kernel(tc, query, key, value, out_0, out_1):
 
         ident = keep.tile([P, P], F32, name="ident")
         make_identity(nc, ident[:])
-        zeros16 = keep.tile([P, 512], BF16, name="zeros16")
+        zeros16 = keep.tile([P, 256], BF16, name="zeros16")
         nc.vector.memset(zeros16[:], 0.0)
         warm = keep.tile([P, 1], F32, name="warm")
         nc.vector.memset(warm[:], 0.0)
@@ -132,15 +129,10 @@ def tile_curveattention_kernel(tc, query, key, value, out_0, out_1):
             else:
                 nc.scalar.copy(out=dst, in_=src)
 
-        def regroup_v(h, c0, c1, eng):
-            if eng == "D":
-                dst = grouped[("v", h)][:, PACK * c0:PACK * c1].rearrange("p (c i t) -> p c t i", i=4, t=PACK)
-                src = raw[("v", h)][:].rearrange("p (t c i) -> p c t i", i=4, t=PACK)[:, c0 // 4:c1 // 4]
-                nc.vector.tensor_copy(out=dst, in_=src)
-            else:
-                dst = grouped[("v", h)][:, PACK * c0:PACK * c1].rearrange("p (c t) -> p c t", t=PACK)
-                src = raw[("v", h)][:].rearrange("p (t c) -> p c t", t=PACK)[:, c0:c1]
-                nc.gpsimd.tensor_scalar(out=dst, in0=src, scalar1=1.0, scalar2=0.0, op0=MULT, op1=ADD)
+        def regroup_v(h, c0, c1):
+            dst = grouped[("v", h)][:, PACK * c0:PACK * c1].rearrange("p (c i t) -> p c t i", i=4, t=PACK)
+            src = raw[("v", h)][:].rearrange("p (t c i) -> p c t i", i=4, t=PACK)[:, c0 // 4:c1 // 4]
+            nc.vector.tensor_copy(out=dst, in_=src)
 
         def mx(out, a, b, h, a0, b0, b1):
             nc.tensor.matmul_mx(
@@ -158,8 +150,8 @@ def tile_curveattention_kernel(tc, query, key, value, out_0, out_1):
         def keep_clock(n):
             nc.tensor.matmul(idle_bank[:, :n], lhsT=zeros[:], rhs=zeros[:, :n], start=True, stop=True)
 
-        for i in range(4):
-            nc.tensor.matmul(idle_bank[:], lhsT=zeros16[:, :P], rhs=zeros16[:], start=True, stop=True)
+        for i in range(8):
+            nc.tensor.matmul(idle_bank[:, :256], lhsT=zeros16[:, :P], rhs=zeros16[:], start=True, stop=True)
 
         def step(kind, nm, i, a, b):
             h, tq = i // NT, i % NT
@@ -170,8 +162,8 @@ def tile_curveattention_kernel(tc, query, key, value, out_0, out_1):
                 flip(nm, i, a, b)
             elif kind == "EA" or kind == "ED":
                 flip_out(nm, i, a, b, kind[1])
-            elif kind == "VP" or kind == "VD":
-                regroup_v(i, a * P, (a + b) * P, kind[1])
+            elif kind == "VD":
+                regroup_v(i, a * P, (a + b) * P)
             elif kind == "QW":
                 quantise("w", h, q0, q0 + b * P)
             elif kind == "Q":

@@ -17,43 +17,13 @@ HEADS = 2
 S = 512
 D = 512
 NT = S // P
+TILES = HEADS * NT
+WORDS = D // 2
+BANK = 512
 FLOPS = 2 * 2 * HEADS * S * S * D
 
 SCALE = D ** (-0.5)
 NEG_LOG_C = -math.log(1.0 + math.exp(math.exp(1.0)))
-
-LOADS = (("q", 0, 0, 1), ("k", 0, 0, 2), ("k", 0, 2, 2), ("q", 0, 1, 3), ("k", 1, 0, 2), ("k", 1, 2, 2), ("v", 0, 0, 4), ("q", 1, 0, 4), ("v", 1, 0, 4))
-
-ORDER = (
-    ("T", "q", 0, 0, 1), ("D", "", 96, 0, 0), ("EA", "q", 0, 0, 1), ("T", "k", 0, 0, 2),
-    ("D", "", 96, 0, 0), ("ED", "k", 0, 0, 2), ("T", "k", 0, 2, 1), ("D", "", 96, 0, 0),
-    ("T", "k", 0, 3, 1), ("EA", "k", 0, 2, 1), ("D", "", 96, 0, 0), ("Q", "q", 0, 0, 1),
-    ("ED", "k", 0, 3, 1), ("T", "q", 0, 1, 1), ("D", "", 96, 0, 0), ("Q", "k", 0, 0, 2),
-    ("T", "q", 0, 2, 2), ("EA", "q", 0, 1, 1), ("Q", "k", 0, 2, 2), ("D", "", 96, 0, 0),
-    ("T", "k", 1, 0, 2), ("ED", "q", 0, 2, 2), ("S", "", 0, 0, 0), ("Q", "q", 0, 1, 1),
-    ("ED", "k", 1, 0, 2), ("XS", "", 0, 0, 0), ("S", "", 1, 0, 0), ("Q", "q", 0, 2, 2),
-    ("ST", "", 0, 0, 0), ("Q", "k", 1, 0, 2), ("XS", "", 1, 0, 0), ("ST", "", 1, 0, 0),
-    ("SW", "", 0, 0, 1), ("VD", "v", 0, 0, 4), ("S", "", 2, 0, 0), ("XST", "", 0, 0, 0),
-    ("T", "k", 1, 2, 2), ("SW", "", 1, 0, 1), ("T", "q", 1, 0, 2), ("XST", "", 1, 0, 0),
-    ("S", "", 3, 0, 0), ("QW", "", 0, 0, 1), ("XS", "", 2, 0, 0), ("T", "q", 1, 2, 2),
-    ("ED", "k", 1, 2, 2), ("EA", "q", 1, 0, 2), ("ST", "", 2, 0, 0), ("Q", "v", 0, 0, 4),
-    ("SW", "", 2, 0, 1), ("XS", "", 3, 0, 0), ("Q", "k", 1, 2, 2), ("QW", "", 1, 0, 1),
-    ("O", "", 0, 0, 0), ("EA", "q", 1, 2, 2), ("Q", "q", 1, 0, 2), ("SW", "", 3, 0, 1),
-    ("O", "", 1, 0, 0), ("EOD", "", 0, 0, 512), ("XST", "", 2, 0, 0), ("S", "", 4, 0, 0),
-    ("S", "", 5, 0, 0), ("EOD", "", 1, 0, 512), ("ST", "", 3, 0, 0), ("XS", "", 4, 0, 0),
-    ("SO", "", 0, 0, 512), ("QW", "", 2, 0, 1), ("Q", "q", 1, 2, 2), ("XS", "", 5, 0, 0),
-    ("SO", "", 1, 0, 512), ("VD", "v", 1, 0, 2), ("O", "", 2, 0, 0), ("SW", "", 4, 0, 1),
-    ("ST", "", 4, 0, 0), ("XST", "", 3, 0, 0), ("S", "", 6, 0, 0), ("SW", "", 5, 0, 1),
-    ("EOD", "", 2, 0, 512), ("ST", "", 5, 0, 0), ("XST", "", 4, 0, 0), ("S", "", 7, 0, 0),
-    ("VD", "v", 1, 2, 2), ("XS", "", 6, 0, 0), ("ST", "", 6, 0, 0), ("SO", "", 2, 0, 512),
-    ("ST", "", 7, 0, 0), ("QW", "", 3, 0, 1), ("XST", "", 5, 0, 0), ("QW", "", 4, 0, 1),
-    ("Q", "v", 1, 0, 4), ("SW", "", 6, 0, 1), ("O", "", 3, 0, 0), ("XS", "", 7, 0, 0),
-    ("QW", "", 5, 0, 1), ("EOD", "", 3, 0, 512), ("XST", "", 6, 0, 0), ("O", "", 4, 0, 0),
-    ("SW", "", 7, 0, 1), ("O", "", 5, 0, 0), ("XST", "", 7, 0, 0), ("EOD", "", 4, 0, 512),
-    ("SO", "", 3, 0, 512), ("EOA", "", 5, 0, 512), ("QW", "", 6, 0, 1), ("QW", "", 7, 0, 1),
-    ("SO", "", 4, 0, 512), ("O", "", 6, 0, 0), ("SO", "", 5, 0, 512), ("O", "", 7, 0, 0),
-    ("EOD", "", 6, 0, 512), ("EOA", "", 7, 0, 512), ("SO", "", 6, 0, 512), ("SO", "", 7, 0, 512),
-)
 
 
 def tile_curveattention_kernel(tc, query, key, value, out_0, out_1):
@@ -61,80 +31,77 @@ def tile_curveattention_kernel(tc, query, key, value, out_0, out_1):
     with ExitStack() as ctx:
         keep = ctx.enter_context(tc.tile_pool(name="keep", bufs=1))
         psum = ctx.enter_context(tc.psum_pool(name="psum", bufs=7))
-        busy = ctx.enter_context(tc.psum_pool(name="busy", bufs=1))
+        filler_psum = ctx.enter_context(tc.psum_pool(name="filler_psum", bufs=1))
         ctx.enter_context(tc.manual_schedule())
 
         ident = keep.tile([P, P], F32, name="ident")
         make_identity(nc, ident[:])
         zeros16 = keep.tile([P, 256], BF16, name="zeros16")
         nc.vector.memset(zeros16[:], 0.0)
-        warm = keep.tile([P, 1], F32, name="warm")
-        nc.vector.memset(warm[:], 0.0)
-        zeros = keep.tile([P, P], F32, name="zeros")
-        nc.vector.memset(zeros[:], 0.0)
-        warm2 = keep.tile([P, 1], F32, name="warm2")
-        nc.scalar.activation(out=warm2[:], in_=warm[:], func=EXP)
+        one_column = keep.tile([P, 1], F32, name="one_column")
+        nc.vector.memset(one_column[:], 0.0)
+        zeros32 = keep.tile([P, P], F32, name="zeros32")
+        nc.vector.memset(zeros32[:], 0.0)
+        table_loaded = keep.tile([P, 1], F32, name="table_loaded")
+        nc.scalar.activation(out=table_loaded[:], in_=one_column[:], func=EXP)
 
-        srcs = {"k": key, "q": query, "v": value}
-        raw = {}
-        grouped = {}
-        codes = {}
-        scales = {}
-        w_out = {}
-        o_out = {}
+        sources = {"q": query, "k": key, "v": value}
+        raw, grouped, codes, scales, w_out, o_out = {}, {}, {}, {}, {}, {}
         for h in range(HEADS):
             for nm in ("k", "q", "v"):
                 raw[(nm, h)] = keep.tile([P, NT * D], BF16, name="raw_%s%d" % (nm, h))
             for nm in ("k", "q", "v", "w"):
-                grouped[(nm, h)] = keep.tile([P, PACK * S], BF16, name="grp_%s%d" % (nm, h), align_bytes=64)
-                codes[(nm, h)] = keep.tile([P, S], U32, name="cod_%s%d" % (nm, h), align_bytes=64)
-                scales[(nm, h)] = keep.tile([P, S], U8, name="scl_%s%d" % (nm, h), align_bytes=64)
+                grouped[(nm, h)] = keep.tile([P, PACK * S], BF16, name="grouped_%s%d" % (nm, h), align_bytes=64)
+                codes[(nm, h)] = keep.tile([P, S], U32, name="codes_%s%d" % (nm, h), align_bytes=64)
+                scales[(nm, h)] = keep.tile([P, S], U8, name="scales_%s%d" % (nm, h), align_bytes=64)
             w_out[h] = keep.tile([P, NT, S], F32, name="w_out%d" % h)
             o_out[h] = keep.tile([P, NT, D], F32, name="o_out%d" % h)
+        bank_of = {}
+        filler_bank = filler_psum.tile([P, BANK], F32, name="filler_bank")
 
-        for nm, h, t0, nt in LOADS:
+        def load(nm, h, t0, nt):
             nc.sync.dma_start(
                 out=raw[(nm, h)][:, t0 * D:(t0 + nt) * D],
-                in_=srcs[nm][0, h].rearrange("(p t) d -> p (t d)", t=NT)[:, t0 * D:(t0 + nt) * D],
+                in_=sources[nm][0, h].rearrange("(p t) d -> p (t d)", t=NT)[:, t0 * D:(t0 + nt) * D],
             )
 
-        banks = {}
+        def hold_clock():
+            nc.tensor.matmul(filler_bank[:, :96], lhsT=zeros32[:], rhs=zeros32[:, :96], start=True, stop=True)
 
-        def quantise(nm, h, c0, c1):
+        def turn(nm, h, t0, nt):
+            words = raw[(nm, h)][:].bitcast(F32)
+            bank = psum.tile([P, nt * WORDS], F32, name="turned", tag="bank")
+            bank_of[(nm, h, t0)] = bank
+            for t in range(nt):
+                for u in range(2):
+                    nc.tensor.transpose(
+                        bank[:, (2 * t + u) * P:(2 * t + u + 1) * P],
+                        words[:, (t0 + t) * WORDS + u * P:(t0 + t) * WORDS + (u + 1) * P],
+                        ident[:],
+                    )
+
+        def copy_turned(copy, nm, h, t0, nt):
+            out = grouped[(nm, h)][:].bitcast(F32)[:, t0 * WORDS:(t0 + nt) * WORDS]
+            copy(
+                out=out.rearrange("p (t r u) -> p t r u", t=nt, u=2),
+                in_=bank_of[(nm, h, t0)][:].rearrange("p (t u r) -> p t r u", t=nt, u=2),
+            )
+
+        def quantise(nm, h, t0, nt):
+            c0, c1 = t0 * P, (t0 + nt) * P
             nc.vector.quantize_mx(
                 out=codes[(nm, h)][:, c0:c1].bitcast(FP8X4),
                 scales=scales[(nm, h)][:, c0:c1],
                 in_=grouped[(nm, h)][:, PACK * c0:PACK * c1],
             )
 
-        def flip(nm, h, t0, nt):
-            words = raw[(nm, h)][:].bitcast(F32)
-            xt = psum.tile([P, nt * 256], F32, name="xt", tag="bank")
-            banks[("T", nm, h, t0)] = xt
-            for tl in range(nt):
-                for u in range(2):
-                    nc.tensor.transpose(
-                        xt[:, (2 * tl + u) * P:(2 * tl + u + 1) * P],
-                        words[:, (t0 + tl) * 256 + u * P:(t0 + tl) * 256 + (u + 1) * P],
-                        ident[:],
-                    )
+        def regroup_value(h, c0, c1):
+            nc.vector.tensor_copy(
+                out=grouped[("v", h)][:, PACK * c0:PACK * c1].rearrange("p (c i t) -> p c t i", i=4, t=PACK),
+                in_=raw[("v", h)][:].rearrange("p (t c i) -> p c t i", i=4, t=PACK)[:, c0 // 4:c1 // 4],
+            )
 
-        def flip_out(nm, h, t0, nt, eng):
-            g32 = grouped[(nm, h)][:].bitcast(F32)
-            xt = banks[("T", nm, h, t0)]
-            dst = g32[:, t0 * 256:(t0 + nt) * 256].rearrange("p (tl c u) -> p tl c u", tl=nt, u=2)
-            src = xt[:].rearrange("p (tl u c) -> p tl c u", tl=nt, u=2)
-            if eng == "D":
-                nc.vector.tensor_copy(out=dst, in_=src)
-            else:
-                nc.scalar.copy(out=dst, in_=src)
-
-        def regroup_v(h, c0, c1):
-            dst = grouped[("v", h)][:, PACK * c0:PACK * c1].rearrange("p (c i t) -> p c t i", i=4, t=PACK)
-            src = raw[("v", h)][:].rearrange("p (t c i) -> p c t i", i=4, t=PACK)[:, c0 // 4:c1 // 4]
-            nc.vector.tensor_copy(out=dst, in_=src)
-
-        def mx(out, a, b, h, a0, b0, b1):
+        def multiply(out, a, b, h, a0, b0, b1):
             nc.tensor.matmul_mx(
                 out=out,
                 lhsT=codes[(a, h)][:, a0:a0 + P].bitcast(FP8X4),
@@ -145,72 +112,129 @@ def tile_curveattention_kernel(tc, query, key, value, out_0, out_1):
                 stop=True,
             )
 
-        idle_bank = busy.tile([P, 512], F32, name="idle_bank")
+        def weights(i):
+            h, t = i // NT, i % NT
+            bank = psum.tile([P, BANK], F32, name="scores", tag="bank")
+            multiply(bank[:], "q", "k", h, t * P, 0, S)
+            nc.scalar.activation(
+                out=w_out[h][:, t, :].rearrange("p (c t) -> p c t", t=NT),
+                in_=bank[:].rearrange("p (t c) -> p c t", t=NT),
+                func=EXP, scale=SCALE, bias=NEG_LOG_C,
+            )
+            nc.sync.dma_start(out=out_1[0, h].rearrange("(p t) k -> p t k", t=NT)[:, t, :], in_=w_out[h][:, t, :])
 
-        def keep_clock(n):
-            nc.tensor.matmul(idle_bank[:, :n], lhsT=zeros[:], rhs=zeros[:, :n], start=True, stop=True)
+        def turned_weights(i):
+            h, q0 = i // NT, (i % NT) * P
+            bank = psum.tile([P, BANK], F32, name="turned_scores", tag="bank")
+            for t in range(NT):
+                multiply(bank[:, t * P:(t + 1) * P], "k", "q", h, t * P, q0, q0 + P)
+            nc.scalar.activation(
+                out=grouped[("w", h)][:, PACK * q0:PACK * (q0 + P)].rearrange("p (c t) -> p c t", t=PACK),
+                in_=bank[:].rearrange("p (t c) -> p c t", t=PACK),
+                func=EXP, scale=SCALE, bias=NEG_LOG_C,
+            )
 
-        for i in range(8):
-            nc.tensor.matmul(idle_bank[:, :256], lhsT=zeros16[:, :P], rhs=zeros16[:], start=True, stop=True)
+        def quantise_weights(i):
+            quantise("w", i // NT, i % NT, 1)
 
-        def step(kind, nm, i, a, b):
-            h, tq = i // NT, i % NT
-            q0 = tq * P
-            if kind == "D":
-                keep_clock(i)
-            elif kind == "T":
-                flip(nm, i, a, b)
-            elif kind == "EA" or kind == "ED":
-                flip_out(nm, i, a, b, kind[1])
-            elif kind == "VD":
-                regroup_v(i, a * P, (a + b) * P)
-            elif kind == "QW":
-                quantise("w", h, q0, q0 + b * P)
-            elif kind == "Q":
-                quantise(nm, i, a * P, (a + b) * P)
-            elif kind == "ST":
-                st = psum.tile([P, 512], F32, name="st", tag="bank")
-                banks[("ST", i)] = st
-                for t in range(NT):
-                    mx(st[:, t * P:(t + 1) * P], "k", "q", h, t * P, q0, q0 + P)
-            elif kind == "SW":
-                nc.sync.dma_start(out=out_1[0, h].rearrange("(p t) k -> p t k", t=NT)[:, tq:tq + b, :], in_=w_out[h][:, tq:tq + b, :])
-            elif kind == "SO2":
-                nc.sync.dma_start(
-                    out=out_0[0, h].rearrange("(p t) d -> p t d", t=NT)[:, tq:tq + b, :],
-                    in_=o_out[h][:, tq:tq + b, :],
-                )
-            elif kind == "SO":
-                nc.sync.dma_start(
-                    out=out_0[0, h].rearrange("(p t) d -> p t d", t=NT)[:, tq, a:a + b],
-                    in_=o_out[h][:, tq, a:a + b],
-                )
-            elif kind == "S":
-                s = psum.tile([P, 512], F32, name="s", tag="bank")
-                banks[("S", i)] = s
-                mx(s[:], "q", "k", h, q0, 0, S)
-            elif kind == "XST":
-                nc.scalar.activation(
-                    out=grouped[("w", h)][:, PACK * q0:PACK * (q0 + P)].rearrange("p (c t) -> p c t", t=PACK),
-                    in_=banks[("ST", i)][:].rearrange("p (t c) -> p c t", t=PACK),
-                    func=EXP, scale=SCALE, bias=NEG_LOG_C,
-                )
-            elif kind == "XS":
-                nc.scalar.activation(
-                    out=w_out[h][:, tq, :].rearrange("p (c t) -> p c t", t=NT),
-                    in_=banks[("S", i)][:].rearrange("p (t c) -> p c t", t=NT),
-                    func=EXP, scale=SCALE, bias=NEG_LOG_C,
-                )
-            elif kind == "EOD":
-                nc.vector.tensor_copy(out=o_out[h][:, tq, a:a + b], in_=banks[("O", i)][:, a:a + b])
-            elif kind == "EOA":
-                nc.scalar.copy(out=o_out[h][:, tq, a:a + b], in_=banks[("O", i)][:, a:a + b])
-            elif kind == "O":
-                o = psum.tile([P, 512], F32, name="o", tag="bank")
-                banks[("O", i)] = o
-                mx(o[:], "w", "v", h, q0, 0, D)
-            else:
-                assert False, kind
+        def product(i):
+            h, t = i // NT, i % NT
+            bank = psum.tile([P, BANK], F32, name="product", tag="bank")
+            bank_of[i] = bank
+            multiply(bank[:], "w", "v", h, t * P, 0, D)
 
-        for kind, nm, i, a, b in ORDER:
-            step(kind, nm, i, a, b)
+        def output(copy, i):
+            h, t = i // NT, i % NT
+            copy(out=o_out[h][:, t, :], in_=bank_of[i][:])
+            nc.sync.dma_start(out=out_0[0, h].rearrange("(p t) d -> p t d", t=NT)[:, t, :], in_=o_out[h][:, t, :])
+
+        by_scalar, by_vector = nc.scalar.copy, nc.vector.tensor_copy
+
+        load("q", 0, 0, 1)
+        load("k", 0, 0, 2)
+        load("k", 0, 2, 2)
+        load("q", 0, 1, 3)
+        load("k", 1, 0, 2)
+        load("k", 1, 2, 2)
+        load("v", 0, 0, 4)
+        load("q", 1, 0, 4)
+        load("v", 1, 0, 4)
+
+        for n in range(8):
+            nc.tensor.matmul(filler_bank[:, :256], lhsT=zeros16[:, :P], rhs=zeros16[:], start=True, stop=True)
+
+        turn("q", 0, 0, 1)
+        hold_clock()
+        copy_turned(by_scalar, "q", 0, 0, 1)
+        turn("k", 0, 0, 2)
+        hold_clock()
+        copy_turned(by_vector, "k", 0, 0, 2)
+        turn("k", 0, 2, 1)
+        hold_clock()
+        copy_turned(by_scalar, "k", 0, 2, 1)
+        quantise("q", 0, 0, 1)
+        turn("k", 0, 3, 1)
+        hold_clock()
+        copy_turned(by_vector, "k", 0, 3, 1)
+        turn("q", 0, 1, 1)
+        hold_clock()
+        copy_turned(by_scalar, "q", 0, 1, 1)
+        quantise("k", 0, 0, 2)
+        quantise("k", 0, 2, 2)
+        turn("q", 0, 2, 2)
+        hold_clock()
+        copy_turned(by_scalar, "q", 0, 2, 2)
+        quantise("q", 0, 1, 1)
+        turn("k", 1, 0, 2)
+        copy_turned(by_vector, "k", 1, 0, 2)
+        quantise("q", 0, 2, 2)
+        quantise("k", 1, 0, 2)
+
+        weights(0)
+        for i in range(TILES):
+            if i + 1 < TILES:
+                weights(i + 1)
+            turned_weights(i)
+            if i == 0:
+                regroup_value(0, 0, D)
+            elif i == 1:
+                turn("k", 1, 2, 2)
+                quantise_weights(0)
+                copy_turned(by_vector, "k", 1, 2, 2)
+                quantise("v", 0, 0, 4)
+                turn("q", 1, 0, 2)
+                copy_turned(by_scalar, "q", 1, 0, 2)
+                quantise("k", 1, 2, 2)
+            elif i == 2:
+                turn("q", 1, 2, 2)
+                copy_turned(by_scalar, "q", 1, 2, 2)
+                quantise_weights(1)
+                quantise("q", 1, 0, 2)
+                product(0)
+                product(1)
+                output(by_vector, 0)
+                output(by_vector, 1)
+                quantise_weights(2)
+                quantise("q", 1, 2, 2)
+            elif i == 4:
+                product(2)
+                regroup_value(1, 0, D // 2)
+                output(by_vector, 2)
+                regroup_value(1, D // 2, D)
+                quantise_weights(3)
+                quantise_weights(4)
+                quantise("v", 1, 0, 4)
+
+        quantise_weights(5)
+        product(3)
+        product(4)
+        product(5)
+        output(by_vector, 3)
+        output(by_vector, 4)
+        output(by_scalar, 5)
+        quantise_weights(6)
+        quantise_weights(7)
+        product(6)
+        product(7)
+        output(by_vector, 6)
+        output(by_scalar, 7)

import math
from contextlib import ExitStack

import concourse.mybir as mybir
from concourse.masks import make_identity

F32 = mybir.dt.float32
BF16 = mybir.dt.bfloat16
U32 = mybir.dt.uint32
U8 = mybir.dt.uint8
FP8X4 = mybir.dt.float8_e4m3fn_x4
EXP = mybir.ActivationFunctionType.Exp

P = 128
PACK = 4
HEADS = 2
S = 512
D = 512
NT = S // P
TILES = HEADS * NT
WORDS = D // 2
BANK = 512
FLOPS = 2 * 2 * HEADS * S * S * D

SCALE = D ** (-0.5)
NEG_LOG_C = -math.log(1.0 + math.exp(math.exp(1.0)))


def tile_curveattention_kernel(tc, query, key, value, out_0, out_1):
    nc = tc.nc
    with ExitStack() as ctx:
        keep = ctx.enter_context(tc.tile_pool(name="keep", bufs=1))
        psum = ctx.enter_context(tc.psum_pool(name="psum", bufs=7))
        filler_psum = ctx.enter_context(tc.psum_pool(name="filler_psum", bufs=1))
        ctx.enter_context(tc.manual_schedule())

        ident = keep.tile([P, P], F32, name="ident")
        make_identity(nc, ident[:])
        zeros16 = keep.tile([P, 256], BF16, name="zeros16")
        nc.vector.memset(zeros16[:], 0.0)
        one_column = keep.tile([P, 1], F32, name="one_column")
        nc.vector.memset(one_column[:], 0.0)
        zeros32 = keep.tile([P, P], F32, name="zeros32")
        nc.vector.memset(zeros32[:], 0.0)
        table_loaded = keep.tile([P, 1], F32, name="table_loaded")
        nc.scalar.activation(out=table_loaded[:], in_=one_column[:], func=EXP)

        sources = {"q": query, "k": key, "v": value}
        raw, grouped, codes, scales, w_out, o_out = {}, {}, {}, {}, {}, {}
        for h in range(HEADS):
            for nm in ("k", "q", "v"):
                raw[(nm, h)] = keep.tile([P, NT * D], BF16, name="raw_%s%d" % (nm, h))
            for nm in ("k", "q", "v", "w"):
                grouped[(nm, h)] = keep.tile([P, PACK * S], BF16, name="grouped_%s%d" % (nm, h), align_bytes=64)
                codes[(nm, h)] = keep.tile([P, S], U32, name="codes_%s%d" % (nm, h), align_bytes=64)
                scales[(nm, h)] = keep.tile([P, S], U8, name="scales_%s%d" % (nm, h), align_bytes=64)
            w_out[h] = keep.tile([P, NT, S], F32, name="w_out%d" % h)
            o_out[h] = keep.tile([P, NT, D], F32, name="o_out%d" % h)
        bank_of = {}
        filler_bank = filler_psum.tile([P, BANK], F32, name="filler_bank")

        def load(nm, h, t0, nt):
            nc.sync.dma_start(
                out=raw[(nm, h)][:, t0 * D:(t0 + nt) * D],
                in_=sources[nm][0, h].rearrange("(p t) d -> p (t d)", t=NT)[:, t0 * D:(t0 + nt) * D],
            )

        def hold_clock():
            nc.tensor.matmul(filler_bank[:, :96], lhsT=zeros32[:], rhs=zeros32[:, :96], start=True, stop=True)

        def turn(nm, h, t0, nt):
            words = raw[(nm, h)][:].bitcast(F32)
            bank = psum.tile([P, nt * WORDS], F32, name="turned", tag="bank")
            bank_of[(nm, h, t0)] = bank
            for t in range(nt):
                for u in range(2):
                    nc.tensor.transpose(
                        bank[:, (2 * t + u) * P:(2 * t + u + 1) * P],
                        words[:, (t0 + t) * WORDS + u * P:(t0 + t) * WORDS + (u + 1) * P],
                        ident[:],
                    )

        def copy_turned(copy, nm, h, t0, nt):
            out = grouped[(nm, h)][:].bitcast(F32)[:, t0 * WORDS:(t0 + nt) * WORDS]
            copy(
                out=out.rearrange("p (t r u) -> p t r u", t=nt, u=2),
                in_=bank_of[(nm, h, t0)][:].rearrange("p (t u r) -> p t r u", t=nt, u=2),
            )

        def quantise(nm, h, t0, nt):
            c0, c1 = t0 * P, (t0 + nt) * P
            nc.vector.quantize_mx(
                out=codes[(nm, h)][:, c0:c1].bitcast(FP8X4),
                scales=scales[(nm, h)][:, c0:c1],
                in_=grouped[(nm, h)][:, PACK * c0:PACK * c1],
            )

        def regroup_value(h, c0, c1):
            nc.vector.tensor_copy(
                out=grouped[("v", h)][:, PACK * c0:PACK * c1].rearrange("p (c i t) -> p c t i", i=4, t=PACK),
                in_=raw[("v", h)][:].rearrange("p (t c i) -> p c t i", i=4, t=PACK)[:, c0 // 4:c1 // 4],
            )

        def multiply(out, a, b, h, a0, b0, b1):
            nc.tensor.matmul_mx(
                out=out,
                lhsT=codes[(a, h)][:, a0:a0 + P].bitcast(FP8X4),
                lhsT_scale=scales[(a, h)][:, a0:a0 + P],
                rhs=codes[(b, h)][:, b0:b1].bitcast(FP8X4),
                rhs_scale=scales[(b, h)][:, b0:b1],
                start=True,
                stop=True,
            )

        def weights(i):
            h, t = i // NT, i % NT
            bank = psum.tile([P, BANK], F32, name="scores", tag="bank")
            multiply(bank[:], "q", "k", h, t * P, 0, S)
            nc.scalar.activation(
                out=w_out[h][:, t, :].rearrange("p (c t) -> p c t", t=NT),
                in_=bank[:].rearrange("p (t c) -> p c t", t=NT),
                func=EXP, scale=SCALE, bias=NEG_LOG_C,
            )
            nc.sync.dma_start(out=out_1[0, h].rearrange("(p t) k -> p t k", t=NT)[:, t, :], in_=w_out[h][:, t, :])

        def turned_weights(i):
            h, q0 = i // NT, (i % NT) * P
            bank = psum.tile([P, BANK], F32, name="turned_scores", tag="bank")
            for t in range(NT):
                multiply(bank[:, t * P:(t + 1) * P], "k", "q", h, t * P, q0, q0 + P)
            nc.scalar.activation(
                out=grouped[("w", h)][:, PACK * q0:PACK * (q0 + P)].rearrange("p (c t) -> p c t", t=PACK),
                in_=bank[:].rearrange("p (t c) -> p c t", t=PACK),
                func=EXP, scale=SCALE, bias=NEG_LOG_C,
            )

        def quantise_weights(i):
            quantise("w", i // NT, i % NT, 1)

        def product(i):
            h, t = i // NT, i % NT
            bank = psum.tile([P, BANK], F32, name="product", tag="bank")
            bank_of[i] = bank
            multiply(bank[:], "w", "v", h, t * P, 0, D)

        def output(copy, i):
            h, t = i // NT, i % NT
            copy(out=o_out[h][:, t, :], in_=bank_of[i][:])
            nc.sync.dma_start(out=out_0[0, h].rearrange("(p t) d -> p t d", t=NT)[:, t, :], in_=o_out[h][:, t, :])

        by_scalar, by_vector = nc.scalar.copy, nc.vector.tensor_copy

        load("q", 0, 0, 1)
        load("k", 0, 0, 2)
        load("k", 0, 2, 2)
        load("q", 0, 1, 3)
        load("k", 1, 0, 2)
        load("k", 1, 2, 2)
        load("v", 0, 0, 4)
        load("q", 1, 0, 4)
        load("v", 1, 0, 4)

        for n in range(8):
            nc.tensor.matmul(filler_bank[:, :256], lhsT=zeros16[:, :P], rhs=zeros16[:], start=True, stop=True)

        turn("q", 0, 0, 1)
        hold_clock()
        copy_turned(by_scalar, "q", 0, 0, 1)
        turn("k", 0, 0, 2)
        hold_clock()
        copy_turned(by_vector, "k", 0, 0, 2)
        turn("k", 0, 2, 1)
        hold_clock()
        copy_turned(by_scalar, "k", 0, 2, 1)
        quantise("q", 0, 0, 1)
        turn("k", 0, 3, 1)
        hold_clock()
        copy_turned(by_vector, "k", 0, 3, 1)
        turn("q", 0, 1, 1)
        hold_clock()
        copy_turned(by_scalar, "q", 0, 1, 1)
        quantise("k", 0, 0, 2)
        quantise("k", 0, 2, 2)
        turn("q", 0, 2, 2)
        hold_clock()
        copy_turned(by_scalar, "q", 0, 2, 2)
        quantise("q", 0, 1, 1)
        turn("k", 1, 0, 2)
        copy_turned(by_vector, "k", 1, 0, 2)
        quantise("q", 0, 2, 2)
        quantise("k", 1, 0, 2)

        weights(0)
        for i in range(TILES):
            if i + 1 < TILES:
                weights(i + 1)
            turned_weights(i)
            if i == 0:
                regroup_value(0, 0, D)
            elif i == 1:
                turn("k", 1, 2, 2)
                quantise_weights(0)
                copy_turned(by_vector, "k", 1, 2, 2)
                quantise("v", 0, 0, 4)
                turn("q", 1, 0, 2)
                copy_turned(by_scalar, "q", 1, 0, 2)
                quantise("k", 1, 2, 2)
            elif i == 2:
                turn("q", 1, 2, 2)
                copy_turned(by_scalar, "q", 1, 2, 2)
                quantise_weights(1)
                quantise("q", 1, 0, 2)
                product(0)
                product(1)
                output(by_vector, 0)
                output(by_vector, 1)
                quantise_weights(2)
                quantise("q", 1, 2, 2)
            elif i == 4:
                product(2)
                regroup_value(1, 0, D // 2)
                output(by_vector, 2)
                regroup_value(1, D // 2, D)
                quantise_weights(3)
                quantise_weights(4)
                quantise("v", 1, 0, 4)

        quantise_weights(5)
        product(3)
        product(4)
        product(5)
        output(by_vector, 3)
        output(by_vector, 4)
        output(by_scalar, 5)
        quantise_weights(6)
        quantise_weights(7)
        product(6)
        product(7)
        output(by_vector, 6)
        output(by_scalar, 7)
